import numpy as np
import ml_dtypes


def mxq(x, axis, fmt="e4m3"):
    dtype, down = {"e4m3": (ml_dtypes.float8_e4m3fn, 7), "e5m2": (ml_dtypes.float8_e5m2, 14)}[fmt]
    v = np.moveaxis(np.asarray(x, np.float32).astype(ml_dtypes.bfloat16).astype(np.float64), axis, -1)
    blocks = v.reshape(v.shape[:-1] + (-1, 32))
    amax = np.abs(blocks).max(-1, keepdims=True)
    byte = np.maximum(np.where(amax > 0, np.frexp(amax)[1] - 1 + 127, 0) - down, 1)
    scale = np.exp2(byte - 127.0)
    codes = (blocks / scale).astype(np.float32).astype(dtype).astype(np.float64)
    return np.moveaxis((codes * scale).reshape(v.shape), -1, axis)


WIDE = False


def mx_kscale(k):
    if not WIDE:
        return np.ones(k)
    levels = np.array([10, -10, 5, -5, 0])
    if k % 512:
        return np.exp2(np.random.permutation(np.resize(levels, k // 32))).repeat(32)
    a = np.empty((k // 512, 16))
    for p in range(k // 512):
        a[p, :8] = np.random.permutation(np.resize(levels, 8))
        for g in range(8):
            far = levels[np.abs(levels - a[p, g]) >= 10]
            a[p, g + 8] = far[np.random.randint(len(far))]
    return np.exp2(a.ravel()).repeat(32)


BF16 = ml_dtypes.bfloat16


def bf(x):
    return np.asarray(x, np.float32).astype(BF16)


def f64(x):
    return np.asarray(x).astype(np.float64)


B, OBS, ACT, U, KSUB = 4096, 383, 128, 1024, 2
DT = 1.0 / KSUB
LN_EPS = 1e-5


def mish(v):
    return v * np.tanh(np.log(1.0 + np.exp(v)))


def layer_norm(v, g, b):
    mu = v.mean(-1, keepdims=True)
    var = np.square(v - mu).mean(-1, keepdims=True)
    return (v - mu) / np.sqrt(var + LN_EPS) * g + b


def setup_inputs():
    s, t = mx_kscale(U), mx_kscale(U)
    return {"h0": bf(np.random.standard_normal((B, U)) * s),
            "z": bf(np.random.standard_normal((B, ACT)) * 0.5),
            "k1": bf(np.random.standard_normal((B, ACT))),
            "W1": bf(np.random.standard_normal((U, U)) / np.sqrt(U) / s[:, None]),
            "b1": bf(np.random.standard_normal(U) * 0.3),
            "ln1_g": bf((1.0 + 0.1 * np.random.standard_normal(U)) * t),
            "ln1_b": bf(0.1 * np.random.standard_normal(U) * t),
            "W2": bf(np.random.standard_normal((U, ACT)) / np.sqrt(U) / t[:, None]),
            "b2": bf(np.random.standard_normal(ACT) * 0.3)}


def reference(h0, z, k1, W1, b1, ln1_g, ln1_b, W2, b2):
    h1 = layer_norm(mish((mxq(f64(h0), 1, "e4m3") @ mxq(f64(W1), 0, "e4m3")) + f64(b1)), f64(ln1_g), f64(ln1_b))
    k2 = (mxq(h1, 1, "e4m3") @ mxq(f64(W2), 0, "e4m3")) + f64(b2)
    return f64(z) + (DT / 2.0) * (f64(k1) + k2)

@@ -1,0 +1,367 @@
+from contextlib import ExitStack
+
+import concourse.mybir as mybir
+from concourse.masks import make_identity
+
+F32 = mybir.dt.float32
+BF16 = mybir.dt.bfloat16
+U32 = mybir.dt.uint32
+U8 = mybir.dt.uint8
+FP8X4 = mybir.dt.float8_e4m3fn_x4
+FUNC = mybir.ActivationFunctionType
+ALU = mybir.AluOpType
+
+P = 128
+BATCH, HID, OUT = 4096, 1024, 128
+TILES = BATCH // P
+QUAD = 4
+QUADS = TILES // QUAD
+PACK = 4
+K_PASS = P * PACK
+PASSES = HID // K_PASS
+BANK = 512
+HALVES = HID // BANK
+U_TILES = HID // P
+LN_EPS = 1e-5
+STEP = 0.25
+
+FLOPS = 2 * BATCH * HID * (HID + OUT)
+
+
+def interleave_four(copy, dst, src):
+    copy(
+        out=dst.rearrange("p (c i) t -> p c t i", i=4),
+        in_=src.rearrange("p t (c i) -> p c t i", i=4),
+    )
+
+
+def tile_actorflowode_pb_t_kernel(tc, h0, z, k1, W1, b1, ln1_g, ln1_b, W2, b2, out):
+    nc = tc.nc
+    h0_rows = h0.rearrange("(p n) k -> p n k", n=TILES)
+    z_rows = z.rearrange("(p n) c -> p n c", n=TILES)
+    k1_rows = k1.rearrange("(p n) c -> p n c", n=TILES)
+    out_rows = out.rearrange("(p n) c -> p n c", n=TILES)
+
+    with ExitStack() as ctx:
+        ctx.enter_context(tc.manual_schedule())
+        keep = ctx.enter_context(tc.tile_pool(name="keep", bufs=1))
+        feed = ctx.enter_context(tc.tile_pool(name="feed", bufs=1))
+        psum = ctx.enter_context(tc.psum_pool(name="psum", bufs=1))
+
+        h0_sb, h0_turned, h0_grouped, h0_codes, h0_scales = {}, {}, {}, {}, {}
+        sums, pre, act, stats, rstd = {}, {}, {}, {}, {}
+        h1, h1_grouped, h1_codes, h1_scales, head, base = {}, {}, {}, {}, {}, {}
+
+        def load_h0(q):
+            h0_sb[q] = feed.tile([P, QUAD, HID], BF16, name="h0_sb", bufs=3)
+            nc.sync.dma_start(out=h0_sb[q][:], in_=h0_rows[:, q * QUAD : (q + 1) * QUAD, :])
+
+        ident = keep.tile([P, P], F32, name="ident")
+        make_identity(nc, ident[:])
+        ones = keep.tile([P, P], BF16, name="ones")
+        nc.vector.memset(ones[:], 1.0)
+        minus_half = keep.tile([P, 1], F32, name="minus_half")
+        nc.vector.memset(minus_half[:], -0.5)
+        bias_row = keep.tile([P, HID + 2 * OUT], BF16, name="bias_row")
+        nc.vector.memset(bias_row[:], 0.0)
+        gain_rows = keep.tile([P, PASSES, PACK], BF16, name="gain_rows")
+        shift_rows = keep.tile([P, PASSES, PACK], BF16, name="shift_rows")
+
+        load_h0(0)
+        nc.scalar.dma_start(out=bias_row[0:1, 0:HID], in_=b1.unsqueeze(0))
+        nc.scalar.dma_start(out=bias_row[0:1, HID : HID + OUT], in_=b2.unsqueeze(0))
+        for rows, vector in ((gain_rows, ln1_g), (shift_rows, ln1_b)):
+            nc.scalar.dma_start(out=rows[:], in_=vector.rearrange("(g p t) -> p g t", p=P, t=PACK))
+
+        def turn_h0(n):
+            words = h0_sb[n // QUAD][:, n % QUAD, :].bitcast(F32)
+            h0_turned[n] = psum.tile([P, PACK, P], F32, name="h0_turned", bufs=1)
+            for g in range(PASSES):
+                for u in range(2):
+                    nc.tensor.transpose(
+                        h0_turned[n][:, 2 * g + u, :],
+                        words[:, 2 * P * g + u : 2 * P * (g + 1) : 2],
+                        ident[:],
+                    )
+
+        def group_h0(n, copy):
+            h0_grouped[n] = feed.tile([P, HID], BF16, name="h0_grouped", bufs=QUAD, align_bytes=64)
+            copy(
+                out=h0_grouped[n][:].bitcast(F32).rearrange("p (g r u) -> p g r u", g=PASSES, u=2),
+                in_=h0_turned[n][:].rearrange("p (g u) r -> p g r u", u=2),
+            )
+
+        def pack_h0(n):
+            h0_codes[n] = feed.tile([P, PASSES * P], U32, name="h0_codes", bufs=2 * QUAD, align_bytes=64)
+            h0_scales[n] = feed.tile([P, PASSES * P], U8, name="h0_scales", bufs=2 * QUAD, align_bytes=64)
+            nc.vector.quantize_mx(
+                out=h0_codes[n][:].bitcast(FP8X4), scales=h0_scales[n][:], in_=h0_grouped[n][:]
+            )
+
+        def first_layer(n):
+            for h in range(HALVES):
+                cols = slice(h * BANK, (h + 1) * BANK)
+                acc = psum.tile([P, BANK], F32, name="acc", bufs=2 * HALVES)
+                sums[n, h] = acc
+                for g in range(PASSES):
+                    rows = slice(g * P, (g + 1) * P)
+                    nc.tensor.matmul_mx(
+                        out=acc[:],
+                        lhsT=h0_codes[n][:, rows].bitcast(FP8X4),
+                        lhsT_scale=h0_scales[n][:, rows],
+                        rhs=w1_codes[:, g, cols].bitcast(FP8X4),
+                        rhs_scale=w1_scales[:, g, cols],
+                        start=(g == 0),
+                        stop=(g == PASSES - 1),
+                    )
+
+        def add_bias(n):
+            pre[n] = work.tile([P, HID], F32, name="pre", bufs=2 * QUAD)
+            for h in range(HALVES):
+                cols = slice(h * BANK, (h + 1) * BANK)
+                nc.vector.tensor_tensor(
+                    out=pre[n][:, cols], in0=sums[n, h][:], in1=b1_all[:, cols], op=ALU.add
+                )
+
+        def exponential(n):
+            act[n] = work.tile([P, HID], F32, name="act", bufs=3 * QUAD)
+            nc.scalar.activation(out=act[n][:], in_=pre[n][:], func=FUNC.Exp)
+
+        def softplus(n):
+            nc.scalar.activation(out=act[n][:], in_=act[n][:], func=FUNC.Ln, bias=1.0)
+
+        def tanh(n):
+            nc.scalar.activation(out=act[n][:], in_=act[n][:], func=FUNC.Tanh)
+
+        def mish_and_statistics(n):
+            nc.vector.tensor_tensor(out=act[n][:], in0=pre[n][:], in1=act[n][:], op=ALU.mult)
+            partial = work.tile([P, HALVES, 6], F32, name="partial", bufs=4)
+            for h in range(HALVES):
+                nc.vector.bn_stats(out=partial[:, h, :], in_=act[n][:, h * BANK : (h + 1) * BANK])
+            stats[n] = work.tile([P, 2], F32, name="stats", bufs=4)
+            nc.vector.bn_aggr(out=stats[n][:], in_=partial[:].rearrange("p h s -> p (h s)"))
+            shifted = work.tile([P, 1], F32, name="shifted", bufs=4)
+            nc.gpsimd.tensor_scalar(
+                out=shifted[:], in0=stats[n][:, 1:2], scalar1=LN_EPS, scalar2=1.0,
+                op0=ALU.add, op1=ALU.mult,
+            )
+            rstd[n] = work.tile([P, 1], F32, name="rstd", bufs=4)
+            nc.gpsimd.tensor_tensor(out=rstd[n][:], in0=shifted[:], in1=minus_half[:], op=ALU.pow)
+
+        def normalise(n):
+            nc.vector.tensor_scalar(
+                out=act[n][:], in0=act[n][:], scalar1=stats[n][:, 0:1], scalar2=rstd[n][:],
+                op0=ALU.subtract, op1=ALU.mult,
+            )
+
+        def turn_and_scale(q, u):
+            if u == 0:
+                h1[q] = work.tile([P, U_TILES, QUAD * P], BF16, name="h1", bufs=2)
+            turned = psum.tile([P, QUAD, P], F32, name="act_turned", bufs=2)
+            for j in range(QUAD):
+                nc.tensor.transpose(
+                    turned[:, j, :], act[q * QUAD + j][:, u * P : (u + 1) * P], ident[:]
+                )
+            nc.scalar.activation(
+                out=h1[q][:, u, :],
+                in_=turned[:].rearrange("p j r -> p (j r)"),
+                func=FUNC.Identity,
+                scale=gains[:, u : u + 1],
+                bias=gains[:, U_TILES + u : U_TILES + u + 1],
+            )
+
+        def group_h1(q, g):
+            h1_grouped[q, g] = work.tile(
+                [P, QUAD * P, PACK], BF16, name="h1_grouped", bufs=PASSES, align_bytes=64
+            )
+            interleave_four(
+                nc.vector.tensor_copy, h1_grouped[q, g][:], h1[q][:, g * PACK : (g + 1) * PACK, :]
+            )
+
+        def pack_h1(q):
+            h1_codes[q] = work.tile([P, PASSES, QUAD * P], U32, name="h1_codes", bufs=2, align_bytes=64)
+            h1_scales[q] = work.tile([P, PASSES, QUAD * P], U8, name="h1_scales", bufs=2, align_bytes=64)
+            for g in range(PASSES):
+                nc.vector.quantize_mx(
+                    out=h1_codes[q][:, g, :].bitcast(FP8X4),
+                    scales=h1_scales[q][:, g, :],
+                    in_=h1_grouped[q, g][:].rearrange("p c t -> p (c t)"),
+                )
+
+        def second_layer(q):
+            head[q] = psum.tile([P, QUAD, OUT], F32, name="head", bufs=1)
+            for j in range(QUAD):
+                rows = slice(j * P, (j + 1) * P)
+                for g in range(PASSES):
+                    nc.tensor.matmul_mx(
+                        out=head[q][:, j, :],
+                        lhsT=h1_codes[q][:, g, rows].bitcast(FP8X4),
+                        lhsT_scale=h1_scales[q][:, g, rows],
+                        rhs=w2_codes[:, g, :].bitcast(FP8X4),
+                        rhs_scale=w2_scales[:, g, :],
+                        start=(g == 0),
+                        stop=(g == PASSES - 1),
+                    )
+
+        def corrector_base(q):
+            tiles = slice(q * QUAD, (q + 1) * QUAD)
+            base[q] = work.tile([P, QUAD, OUT], F32, name="base", bufs=2)
+            nc.vector.scalar_tensor_tensor(
+                out=base[q][:], in0=k1_sb[:, tiles, :], scalar=STEP, in1=z_sb[:, tiles, :],
+                op0=ALU.mult, op1=ALU.add,
+            )
+            nc.vector.tensor_tensor(
+                out=base[q][:], in0=base[q][:],
+                in1=b2_step[:].unsqueeze(1).to_broadcast([P, QUAD, OUT]), op=ALU.add,
+            )
+
+        def corrector(q):
+            result = work.tile([P, QUAD, OUT], F32, name="result", bufs=2)
+            nc.vector.scalar_tensor_tensor(
+                out=result[:], in0=head[q][:], scalar=STEP, in1=base[q][:],
+                op0=ALU.mult, op1=ALU.add,
+            )
+            nc.sync.dma_start(out=out_rows[:, q * QUAD : (q + 1) * QUAD, :], in_=result[:])
+
+        w1_codes = keep.tile([P, PASSES, HID], U32, name="w1_codes", align_bytes=64)
+        w1_scales = keep.tile([P, PASSES, HID], U8, name="w1_scales", align_bytes=64)
+        w2_codes = keep.tile([P, PASSES, OUT], U32, name="w2_codes", align_bytes=64)
+        w2_scales = keep.tile([P, PASSES, OUT], U8, name="w2_scales", align_bytes=64)
+        b1_all = keep.tile([P, HID], F32, name="b1_all")
+        b2_step = keep.tile([P, OUT], F32, name="b2_step")
+        gains = keep.tile([P, 2 * U_TILES], F32, name="gains")
+        z_sb = keep.tile([P, TILES, OUT], BF16, name="z_sb")
+        k1_sb = keep.tile([P, TILES, OUT], BF16, name="k1_sb")
+
+        with tc.tile_pool(name="prep", bufs=1) as prep:
+            w1_raw = prep.tile([P, PASSES, PACK, HID], BF16, name="w1_raw")
+            for g in range(PASSES):
+                nc.sync.dma_start(
+                    out=w1_raw[:, g, :, :],
+                    in_=W1[g * K_PASS : (g + 1) * K_PASS, :].rearrange("(p t) c -> p t c", t=PACK),
+                )
+            w2_raw = prep.tile([P, PASSES, PACK, OUT], BF16, name="w2_raw")
+            nc.scalar.dma_start(
+                out=w2_raw[:], in_=W2.rearrange("(g p t) c -> p g t c", p=P, t=PACK)
+            )
+            load_h0(1)
+            nc.sync.dma_start(out=z_sb[:], in_=z_rows)
+            nc.sync.dma_start(out=k1_sb[:], in_=k1_rows)
+
+            for h in range(HALVES):
+                cols = slice(h * BANK, (h + 1) * BANK)
+                spread = psum.tile([P, BANK], F32, name="acc", bufs=4)
+                nc.tensor.matmul(out=spread[:], lhsT=ones[:], rhs=bias_row[:, cols], start=True, stop=True)
+                nc.scalar.copy(
+                    out=b1_all[:, cols].rearrange("p (t m) -> p t m", t=PACK),
+                    in_=spread[:].rearrange("p (m t) -> p t m", t=PACK),
+                )
+            spread = psum.tile([P, BANK], F32, name="acc", bufs=4)
+            nc.tensor.matmul(
+                out=spread[:, 0 : 2 * OUT], lhsT=ones[:], rhs=bias_row[:, HID : HID + 2 * OUT],
+                start=True, stop=True,
+            )
+            nc.scalar.mul(out=b2_step[:], in_=spread[:, 0:OUT], mul=STEP)
+            for v, rows in enumerate((gain_rows, shift_rows)):
+                nc.vector.tensor_copy(
+                    out=gains[:, v * U_TILES : (v + 1) * U_TILES],
+                    in_=rows[:].rearrange("p g t -> p (g t)"),
+                )
+
+            w1_grouped = {}
+            for g in range(PASSES):
+                pair = range(g * QUAD // PASSES, (g + 1) * QUAD // PASSES)
+                for n in pair:
+                    turn_h0(n)
+                    group_h0(n, nc.scalar.copy)
+                for h in range(HALVES):
+                    w1_grouped[g, h] = prep.tile(
+                        [P, BANK, PACK], BF16, name="w1_grouped", bufs=PASSES * HALVES, align_bytes=64
+                    )
+                    copy = nc.vector.tensor_copy if h == 0 else nc.scalar.copy
+                    copy(
+                        out=w1_grouped[g, h][:].rearrange("p (t m) j -> p t m j", t=PACK),
+                        in_=w1_raw[:, g, :, h * BANK : (h + 1) * BANK].rearrange(
+                            "p j (m t) -> p t m j", t=PACK
+                        ),
+                    )
+                for n in pair:
+                    pack_h0(n)
+            for h in range(HALVES):
+                for g in range(PASSES):
+                    cols = slice(h * BANK, (h + 1) * BANK)
+                    nc.vector.quantize_mx(
+                        out=w1_codes[:, g, cols].bitcast(FP8X4),
+                        scales=w1_scales[:, g, cols],
+                        in_=w1_grouped[g, h][:].rearrange("p c t -> p (c t)"),
+                    )
+            w2_grouped = prep.tile([P, PASSES, OUT, PACK], BF16, name="w2_grouped", align_bytes=64)
+            for g in range(PASSES):
+                interleave_four(
+                    nc.vector.tensor_copy, w2_grouped[:, g, :, :], w2_raw[:, g, :, :]
+                )
+            nc.vector.quantize_mx(
+                out=w2_codes[:].rearrange("p g c -> p (g c)").bitcast(FP8X4),
+                scales=w2_scales[:].rearrange("p g c -> p (g c)"),
+                in_=w2_grouped[:].rearrange("p g c t -> p (g c t)"),
+            )
+
+        work = ctx.enter_context(tc.tile_pool(name="work", bufs=1))
+        banks_a_tile = U_TILES // QUAD
+        ahead = 2
+        SCALAR_COPIES = 3
+
+        def live(q):
+            return 0 <= q < QUADS
+
+        for i in range(-1, QUADS + 2):
+            if live(i + 3):
+                load_h0(i + 3)
+            early = SCALAR_COPIES if live(i - 1) else 0
+            for j in range(QUAD):
+                if live(i - 1):
+                    tanh((i - 1) * QUAD + j)
+                if live(i - 2):
+                    for u in range(j * banks_a_tile, (j + 1) * banks_a_tile):
+                        turn_and_scale(i - 2, u)
+                if live(i + 2) and j < early:
+                    turn_h0((i + 2) * QUAD + j)
+                    group_h0((i + 2) * QUAD + j, nc.scalar.copy)
+            if live(i - 1):
+                for n in range((i - 1) * QUAD, i * QUAD):
+                    mish_and_statistics(n)
+                    if n > (i - 1) * QUAD:
+                        normalise(n - 1)
+            if live(i):
+                for n in range(i * QUAD, (i + 1) * QUAD):
+                    exponential(n)
+                for n in range(i * QUAD, (i + 1) * QUAD):
+                    softplus(n)
+            if live(i + 1):
+                for j in range(ahead):
+                    first_layer((i + 1) * QUAD + j)
+            if live(i + 2) and early < QUAD:
+                turn_h0((i + 2) * QUAD + early)
+            if live(i - 2):
+                corrector_base(i - 2)
+                group_h1(i - 2, 0)
+            if live(i - 1):
+                normalise(i * QUAD - 1)
+            if live(i - 2):
+                group_h1(i - 2, 1)
+                pack_h1(i - 2)
+                second_layer(i - 2)
+            for j in range(QUAD):
+                if live(i + 1):
+                    add_bias((i + 1) * QUAD + j)
+                    if j + ahead < QUAD:
+                        first_layer((i + 1) * QUAD + j + ahead)
+                if live(i + 2) and j >= early:
+                    group_h0((i + 2) * QUAD + j, nc.vector.tensor_copy)
+                    if j + 1 < QUAD:
+                        turn_h0((i + 2) * QUAD + j + 1)
+            if live(i + 2):
+                for n in range((i + 2) * QUAD, (i + 3) * QUAD):
+                    pack_h0(n)
+            if live(i - 2):
+                corrector(i - 2)

@@ -21,6 +21,11 @@ K_PASS = P * PACK
 PASSES = HID // K_PASS
 BANK = 512
 HALVES = HID // BANK
+LOAD = 2
+ACC = 3
+TURNED = 4
+LOADS = 4
+GROUP = 8
 U_TILES = HID // P
 LN_EPS = 1e-5
 STEP = 0.25
@@ -48,34 +53,39 @@ def tile_actorflowode_pb_t_kernel(tc, h0, z, k1, W1, b1, ln1_g, ln1_b, W2, b2, o
         feed = ctx.enter_context(tc.tile_pool(name="feed", bufs=1))
         psum = ctx.enter_context(tc.psum_pool(name="psum", bufs=1))
 
+        LEAD = 4
+        state, act_turned, base_bank = {}, {}, {}
         h0_sb, h0_turned, h0_grouped, h0_codes, h0_scales = {}, {}, {}, {}, {}
-        sums, pre, act, stats, rstd = {}, {}, {}, {}, {}
+        sums, pre, act, partial, stats, rstd = {}, {}, {}, {}, {}, {}
         h1, h1_grouped, h1_codes, h1_scales, head, base = {}, {}, {}, {}, {}, {}
 
-        def load_h0(q):
-            h0_sb[q] = feed.tile([P, QUAD, HID], BF16, name="h0_sb", bufs=3)
-            nc.sync.dma_start(out=h0_sb[q][:], in_=h0_rows[:, q * QUAD : (q + 1) * QUAD, :])
+        def load_h0(first, count):
+            rows = feed.tile([P, LOAD, HID], BF16, name="h0_sb", bufs=LOADS)
+            nc.sync.dma_start(out=rows[:, 0:count, :], in_=h0_rows[:, first : first + count, :])
+            for j in range(count):
+                h0_sb[first + j] = rows[:, j, :]
 
         ident = keep.tile([P, P], F32, name="ident")
         make_identity(nc, ident[:])
+        ident_bf16 = keep.tile([P, P], BF16, name="ident_bf16")
+        make_identity(nc, ident_bf16[:])
         ones = keep.tile([P, P], BF16, name="ones")
         nc.vector.memset(ones[:], 1.0)
         minus_half = keep.tile([P, 1], F32, name="minus_half")
         nc.vector.memset(minus_half[:], -0.5)
-        bias_row = keep.tile([P, HID + 2 * OUT], BF16, name="bias_row")
+        bias_row = keep.tile([P, HID + OUT], BF16, name="bias_row")
         nc.vector.memset(bias_row[:], 0.0)
         gain_rows = keep.tile([P, PASSES, PACK], BF16, name="gain_rows")
         shift_rows = keep.tile([P, PASSES, PACK], BF16, name="shift_rows")
 
-        load_h0(0)
         nc.scalar.dma_start(out=bias_row[0:1, 0:HID], in_=b1.unsqueeze(0))
         nc.scalar.dma_start(out=bias_row[0:1, HID : HID + OUT], in_=b2.unsqueeze(0))
         for rows, vector in ((gain_rows, ln1_g), (shift_rows, ln1_b)):
             nc.scalar.dma_start(out=rows[:], in_=vector.rearrange("(g p t) -> p g t", p=P, t=PACK))
 
         def turn_h0(n):
-            words = h0_sb[n // QUAD][:, n % QUAD, :].bitcast(F32)
-            h0_turned[n] = psum.tile([P, PACK, P], F32, name="h0_turned", bufs=1)
+            words = h0_sb[n].bitcast(F32)
+            h0_turned[n] = psum.tile([P, PACK, P], F32, name="turned", bufs=TURNED)
             for g in range(PASSES):
                 for u in range(2):
                     nc.tensor.transpose(
@@ -83,17 +93,19 @@ def tile_actorflowode_pb_t_kernel(tc, h0, z, k1, W1, b1, ln1_g, ln1_b, W2, b2, o
                         words[:, 2 * P * g + u : 2 * P * (g + 1) : 2],
                         ident[:],
                     )
+            if (n + 1) % LOAD == 0 and n + 1 + (LOADS - 1) * LOAD < TILES:
+                load_h0(n + 1 + (LOADS - 1) * LOAD, LOAD)
 
         def group_h0(n, copy):
-            h0_grouped[n] = feed.tile([P, HID], BF16, name="h0_grouped", bufs=QUAD, align_bytes=64)
+            h0_grouped[n] = feed.tile([P, HID], BF16, name="h0_grouped", bufs=4, align_bytes=64)
             copy(
                 out=h0_grouped[n][:].bitcast(F32).rearrange("p (g r u) -> p g r u", g=PASSES, u=2),
                 in_=h0_turned[n][:].rearrange("p (g u) r -> p g r u", u=2),
             )
 
         def pack_h0(n):
-            h0_codes[n] = feed.tile([P, PASSES * P], U32, name="h0_codes", bufs=2 * QUAD, align_bytes=64)
-            h0_scales[n] = feed.tile([P, PASSES * P], U8, name="h0_scales", bufs=2 * QUAD, align_bytes=64)
+            h0_codes[n] = feed.tile([P, PASSES * P], U32, name="h0_codes", bufs=4, align_bytes=64)
+            h0_scales[n] = feed.tile([P, PASSES * P], U8, name="h0_scales", bufs=4, align_bytes=64)
             nc.vector.quantize_mx(
                 out=h0_codes[n][:].bitcast(FP8X4), scales=h0_scales[n][:], in_=h0_grouped[n][:]
             )
@@ -101,7 +113,7 @@ def tile_actorflowode_pb_t_kernel(tc, h0, z, k1, W1, b1, ln1_g, ln1_b, W2, b2, o
         def first_layer(n):
             for h in range(HALVES):
                 cols = slice(h * BANK, (h + 1) * BANK)
-                acc = psum.tile([P, BANK], F32, name="acc", bufs=2 * HALVES)
+                acc = psum.tile([P, BANK], F32, name="acc", bufs=ACC)
                 sums[n, h] = acc
                 for g in range(PASSES):
                     rows = slice(g * P, (g + 1) * P)
@@ -116,7 +128,7 @@ def tile_actorflowode_pb_t_kernel(tc, h0, z, k1, W1, b1, ln1_g, ln1_b, W2, b2, o
                     )
 
         def add_bias(n):
-            pre[n] = work.tile([P, HID], F32, name="pre", bufs=2 * QUAD)
+            pre[n] = work.tile([P, HID], F32, name="pre", bufs=13)
             for h in range(HALVES):
                 cols = slice(h * BANK, (h + 1) * BANK)
                 nc.vector.tensor_tensor(
@@ -124,7 +136,7 @@ def tile_actorflowode_pb_t_kernel(tc, h0, z, k1, W1, b1, ln1_g, ln1_b, W2, b2, o
                 )
 
         def exponential(n):
-            act[n] = work.tile([P, HID], F32, name="act", bufs=3 * QUAD)
+            act[n] = work.tile([P, HID], F32, name="act", bufs=22)
             nc.scalar.activation(out=act[n][:], in_=pre[n][:], func=FUNC.Exp)
 
         def softplus(n):
@@ -133,13 +145,19 @@ def tile_actorflowode_pb_t_kernel(tc, h0, z, k1, W1, b1, ln1_g, ln1_b, W2, b2, o
         def tanh(n):
             nc.scalar.activation(out=act[n][:], in_=act[n][:], func=FUNC.Tanh)
 
-        def mish_and_statistics(n):
+        def mish(n):
             nc.vector.tensor_tensor(out=act[n][:], in0=pre[n][:], in1=act[n][:], op=ALU.mult)
-            partial = work.tile([P, HALVES, 6], F32, name="partial", bufs=4)
+
+        def partial_statistics(n):
+            partial[n] = work.tile([P, HALVES, 6], F32, name="partial", bufs=4)
             for h in range(HALVES):
-                nc.vector.bn_stats(out=partial[:, h, :], in_=act[n][:, h * BANK : (h + 1) * BANK])
+                nc.vector.bn_stats(
+                    out=partial[n][:, h, :], in_=act[n][:, h * BANK : (h + 1) * BANK]
+                )
+
+        def statistics(n):
             stats[n] = work.tile([P, 2], F32, name="stats", bufs=4)
-            nc.vector.bn_aggr(out=stats[n][:], in_=partial[:].rearrange("p h s -> p (h s)"))
+            nc.vector.bn_aggr(out=stats[n][:], in_=partial[n][:].rearrange("p h s -> p (h s)"))
             shifted = work.tile([P, 1], F32, name="shifted", bufs=4)
             nc.gpsimd.tensor_scalar(
                 out=shifted[:], in0=stats[n][:, 1:2], scalar1=LN_EPS, scalar2=1.0,
@@ -154,126 +172,146 @@ def tile_actorflowode_pb_t_kernel(tc, h0, z, k1, W1, b1, ln1_g, ln1_b, W2, b2, o
                 op0=ALU.subtract, op1=ALU.mult,
             )
 
-        def turn_and_scale(q, u):
-            if u == 0:
-                h1[q] = work.tile([P, U_TILES, QUAD * P], BF16, name="h1", bufs=2)
-            turned = psum.tile([P, QUAD, P], F32, name="act_turned", bufs=2)
-            for j in range(QUAD):
-                nc.tensor.transpose(
-                    turned[:, j, :], act[q * QUAD + j][:, u * P : (u + 1) * P], ident[:]
-                )
-            nc.scalar.activation(
-                out=h1[q][:, u, :],
-                in_=turned[:].rearrange("p j r -> p (j r)"),
-                func=FUNC.Identity,
-                scale=gains[:, u : u + 1],
-                bias=gains[:, U_TILES + u : U_TILES + u + 1],
-            )
+        def turn_act(unit, bank):
+            blocks = BANK // (len(unit) * P)
+            turned = psum.tile([P, blocks, len(unit), P], F32, name="turned", bufs=TURNED)
+            act_turned[unit, bank] = turned
+            for b in range(blocks):
+                u = bank * blocks + b
+                for j, n in enumerate(unit):
+                    nc.tensor.transpose(turned[:, b, j, :], act[n][:, u * P : (u + 1) * P], ident[:])
 
-        def group_h1(q, g):
-            h1_grouped[q, g] = work.tile(
-                [P, QUAD * P, PACK], BF16, name="h1_grouped", bufs=PASSES, align_bytes=64
-            )
-            interleave_four(
-                nc.vector.tensor_copy, h1_grouped[q, g][:], h1[q][:, g * PACK : (g + 1) * PACK, :]
-            )
-
-        def pack_h1(q):
-            h1_codes[q] = work.tile([P, PASSES, QUAD * P], U32, name="h1_codes", bufs=2, align_bytes=64)
-            h1_scales[q] = work.tile([P, PASSES, QUAD * P], U8, name="h1_scales", bufs=2, align_bytes=64)
-            for g in range(PASSES):
-                nc.vector.quantize_mx(
-                    out=h1_codes[q][:, g, :].bitcast(FP8X4),
-                    scales=h1_scales[q][:, g, :],
-                    in_=h1_grouped[q, g][:].rearrange("p c t -> p (c t)"),
+        def scale_act(unit, bank):
+            width = len(unit) * P
+            blocks = BANK // width
+            if bank * blocks % PACK == 0:
+                h1[unit, bank * blocks // PACK] = work.tile([P, PACK, width], BF16, name="h1", bufs=3)
+            for b in range(blocks):
+                u = bank * blocks + b
+                nc.scalar.activation(
+                    out=h1[unit, u // PACK][:, u % PACK, :],
+                    in_=act_turned[unit, bank][:, b, :, :].rearrange("p j r -> p (j r)"),
+                    func=FUNC.Identity,
+                    scale=gains[:, u : u + 1],
+                    bias=gains[:, U_TILES + u : U_TILES + u + 1],
                 )
 
-        def second_layer(q):
-            head[q] = psum.tile([P, QUAD, OUT], F32, name="head", bufs=1)
-            for j in range(QUAD):
+        def group_h1(unit, g):
+            h1_grouped[unit, g] = work.tile(
+                [P, len(unit) * P, PACK], BF16, name="h1_grouped", bufs=PASSES, align_bytes=64
+            )
+            interleave_four(nc.vector.tensor_copy, h1_grouped[unit, g][:], h1[unit, g][:])
+
+        def pack_h1(unit, g):
+            width = len(unit) * P
+            h1_codes[unit, g] = work.tile([P, width], U32, name="h1_codes", bufs=3, align_bytes=64)
+            h1_scales[unit, g] = work.tile([P, width], U8, name="h1_scales", bufs=3, align_bytes=64)
+            nc.vector.quantize_mx(
+                out=h1_codes[unit, g][:].bitcast(FP8X4),
+                scales=h1_scales[unit, g][:],
+                in_=h1_grouped[unit, g][:].rearrange("p c t -> p (c t)"),
+            )
+
+        def second_layer(unit):
+            head[unit] = psum.tile([P, len(unit), OUT], F32, name="head", bufs=1)
+            for j in range(len(unit)):
                 rows = slice(j * P, (j + 1) * P)
                 for g in range(PASSES):
                     nc.tensor.matmul_mx(
-                        out=head[q][:, j, :],
-                        lhsT=h1_codes[q][:, g, rows].bitcast(FP8X4),
-                        lhsT_scale=h1_scales[q][:, g, rows],
+                        out=head[unit][:, j, :],
+                        lhsT=h1_codes[unit, g][:, rows].bitcast(FP8X4),
+                        lhsT_scale=h1_scales[unit, g][:, rows],
                         rhs=w2_codes[:, g, :].bitcast(FP8X4),
                         rhs_scale=w2_scales[:, g, :],
                         start=(g == 0),
                         stop=(g == PASSES - 1),
                     )
 
-        def corrector_base(q):
-            tiles = slice(q * QUAD, (q + 1) * QUAD)
-            base[q] = work.tile([P, QUAD, OUT], F32, name="base", bufs=2)
-            nc.vector.scalar_tensor_tensor(
-                out=base[q][:], in0=k1_sb[:, tiles, :], scalar=STEP, in1=z_sb[:, tiles, :],
-                op0=ALU.mult, op1=ALU.add,
-            )
-            nc.vector.tensor_tensor(
-                out=base[q][:], in0=base[q][:],
-                in1=b2_step[:].unsqueeze(1).to_broadcast([P, QUAD, OUT]), op=ALU.add,
-            )
+        def load_base(unit):
+            tiles = slice(unit[0], unit[-1] + 1)
+            for name, rows in (("z", z_rows), ("k1", k1_rows)):
+                state[name, unit] = work.tile([P, len(unit), OUT], BF16, name="state_" + name, bufs=2)
+                nc.sync.dma_start(out=state[name, unit][:], in_=rows[:, tiles, :])
 
-        def corrector(q):
-            result = work.tile([P, QUAD, OUT], F32, name="result", bufs=2)
+        def add_base(unit):
+            width = len(unit) * OUT
+            bank = psum.tile([P, len(unit), OUT], F32, name="head", bufs=1)
+            flat = bank[:].rearrange("p j c -> p (j c)")
+            nc.tensor.matmul(
+                out=flat, lhsT=ident_bf16[:], rhs=state["z", unit][:].rearrange("p j c -> p (j c)"),
+                start=True, stop=False,
+            )
+            nc.tensor.matmul(
+                out=flat, lhsT=quarter[:], rhs=state["k1", unit][:].rearrange("p j c -> p (j c)"),
+                start=False, stop=False,
+            )
+            nc.tensor.matmul(
+                out=flat, lhsT=quarter_ones[:], rhs=b2_rows[:, 0:width], start=False, stop=True
+            )
+            base_bank[unit] = bank
+
+        def copy_base(unit):
+            base[unit] = work.tile([P, len(unit), OUT], F32, name="base", bufs=3)
+            nc.scalar.copy(out=base[unit][:], in_=base_bank[unit][:])
+
+        def corrector(unit):
+            result = work.tile([P, len(unit), OUT], F32, name="result", bufs=2)
             nc.vector.scalar_tensor_tensor(
-                out=result[:], in0=head[q][:], scalar=STEP, in1=base[q][:],
+                out=result[:], in0=head[unit][:], scalar=STEP, in1=base[unit][:],
                 op0=ALU.mult, op1=ALU.add,
             )
-            nc.sync.dma_start(out=out_rows[:, q * QUAD : (q + 1) * QUAD, :], in_=result[:])
+            nc.sync.dma_start(out=out_rows[:, unit[0] : unit[-1] + 1, :], in_=result[:])
 
         w1_codes = keep.tile([P, PASSES, HID], U32, name="w1_codes", align_bytes=64)
         w1_scales = keep.tile([P, PASSES, HID], U8, name="w1_scales", align_bytes=64)
         w2_codes = keep.tile([P, PASSES, OUT], U32, name="w2_codes", align_bytes=64)
         w2_scales = keep.tile([P, PASSES, OUT], U8, name="w2_scales", align_bytes=64)
         b1_all = keep.tile([P, HID], F32, name="b1_all")
-        b2_step = keep.tile([P, OUT], F32, name="b2_step")
         gains = keep.tile([P, 2 * U_TILES], F32, name="gains")
-        z_sb = keep.tile([P, TILES, OUT], BF16, name="z_sb")
-        k1_sb = keep.tile([P, TILES, OUT], BF16, name="k1_sb")
+        quarter = keep.tile([P, P], BF16, name="quarter")
+        quarter_ones = keep.tile([P, P], BF16, name="quarter_ones")
+        b2_rows = keep.tile([P, QUAD * OUT], BF16, name="b2_rows")
 
         with tc.tile_pool(name="prep", bufs=1) as prep:
-            w1_raw = prep.tile([P, PASSES, PACK, HID], BF16, name="w1_raw")
+            w1_raw = {}
             for g in range(PASSES):
+                w1_raw[g] = prep.tile([P, PACK, HID], BF16, name="w1_raw", bufs=PASSES)
                 nc.sync.dma_start(
-                    out=w1_raw[:, g, :, :],
+                    out=w1_raw[g][:],
                     in_=W1[g * K_PASS : (g + 1) * K_PASS, :].rearrange("(p t) c -> p t c", t=PACK),
                 )
             w2_raw = prep.tile([P, PASSES, PACK, OUT], BF16, name="w2_raw")
             nc.scalar.dma_start(
                 out=w2_raw[:], in_=W2.rearrange("(g p t) c -> p g t c", p=P, t=PACK)
             )
-            load_h0(1)
-            nc.sync.dma_start(out=z_sb[:], in_=z_rows)
-            nc.sync.dma_start(out=k1_sb[:], in_=k1_rows)
+            for first in range(0, LOADS * LOAD, LOAD):
+                load_h0(first, LOAD)
 
+            nc.vector.tensor_scalar_mul(quarter[:], ident_bf16[:], STEP)
+            nc.vector.memset(quarter_ones[:], STEP)
             for h in range(HALVES):
                 cols = slice(h * BANK, (h + 1) * BANK)
-                spread = psum.tile([P, BANK], F32, name="acc", bufs=4)
+                spread = psum.tile([P, BANK], F32, name="acc", bufs=ACC)
                 nc.tensor.matmul(out=spread[:], lhsT=ones[:], rhs=bias_row[:, cols], start=True, stop=True)
                 nc.scalar.copy(
                     out=b1_all[:, cols].rearrange("p (t m) -> p t m", t=PACK),
                     in_=spread[:].rearrange("p (m t) -> p t m", t=PACK),
                 )
-            spread = psum.tile([P, BANK], F32, name="acc", bufs=4)
-            nc.tensor.matmul(
-                out=spread[:, 0 : 2 * OUT], lhsT=ones[:], rhs=bias_row[:, HID : HID + 2 * OUT],
-                start=True, stop=True,
-            )
-            nc.scalar.mul(out=b2_step[:], in_=spread[:, 0:OUT], mul=STEP)
+            for j in range(QUAD):
+                nc.vector.tensor_copy(
+                    out=b2_rows[:, j * OUT : (j + 1) * OUT], in_=bias_row[:, HID : HID + OUT]
+                )
             for v, rows in enumerate((gain_rows, shift_rows)):
                 nc.vector.tensor_copy(
                     out=gains[:, v * U_TILES : (v + 1) * U_TILES],
                     in_=rows[:].rearrange("p g t -> p (g t)"),
                 )
 
+            turn_h0(0)
+            turn_h0(1)
             w1_grouped = {}
+            w2_grouped = prep.tile([P, PASSES, OUT, PACK], BF16, name="w2_grouped", align_bytes=64)
             for g in range(PASSES):
-                pair = range(g * QUAD // PASSES, (g + 1) * QUAD // PASSES)
-                for n in pair:
-                    turn_h0(n)
-                    group_h0(n, nc.scalar.copy)
                 for h in range(HALVES):
                     w1_grouped[g, h] = prep.tile(
                         [P, BANK, PACK], BF16, name="w1_grouped", bufs=PASSES * HALVES, align_bytes=64
@@ -281,12 +319,15 @@ def tile_actorflowode_pb_t_kernel(tc, h0, z, k1, W1, b1, ln1_g, ln1_b, W2, b2, o
                     copy = nc.vector.tensor_copy if h == 0 else nc.scalar.copy
                     copy(
                         out=w1_grouped[g, h][:].rearrange("p (t m) j -> p t m j", t=PACK),
-                        in_=w1_raw[:, g, :, h * BANK : (h + 1) * BANK].rearrange(
+                        in_=w1_raw[g][:, :, h * BANK : (h + 1) * BANK].rearrange(
                             "p j (m t) -> p t m j", t=PACK
                         ),
                     )
-                for n in pair:
-                    pack_h0(n)
+            for n in range(2):
+                group_h0(n, nc.vector.tensor_copy)
+            for n in range(2, 6):
+                turn_h0(n)
+                group_h0(n, nc.scalar.copy)
             for h in range(HALVES):
                 for g in range(PASSES):
                     cols = slice(h * BANK, (h + 1) * BANK)
@@ -295,73 +336,117 @@ def tile_actorflowode_pb_t_kernel(tc, h0, z, k1, W1, b1, ln1_g, ln1_b, W2, b2, o
                         scales=w1_scales[:, g, cols],
                         in_=w1_grouped[g, h][:].rearrange("p c t -> p (c t)"),
                     )
-            w2_grouped = prep.tile([P, PASSES, OUT, PACK], BF16, name="w2_grouped", align_bytes=64)
+                pack_h0(h)
             for g in range(PASSES):
-                interleave_four(
-                    nc.vector.tensor_copy, w2_grouped[:, g, :, :], w2_raw[:, g, :, :]
-                )
+                interleave_four(nc.vector.tensor_copy, w2_grouped[:, g, :, :], w2_raw[:, g, :, :])
             nc.vector.quantize_mx(
                 out=w2_codes[:].rearrange("p g c -> p (g c)").bitcast(FP8X4),
                 scales=w2_scales[:].rearrange("p g c -> p (g c)"),
                 in_=w2_grouped[:].rearrange("p g c t -> p (g c t)"),
             )
-
         work = ctx.enter_context(tc.tile_pool(name="work", bufs=1))
-        banks_a_tile = U_TILES // QUAD
-        ahead = 2
-        SCALAR_COPIES = 3
 
-        def live(q):
-            return 0 <= q < QUADS
+        def live(n):
+            return 0 <= n < TILES
 
-        for i in range(-1, QUADS + 2):
-            if live(i + 3):
-                load_h0(i + 3)
-            early = SCALAR_COPIES if live(i - 1) else 0
-            for j in range(QUAD):
-                if live(i - 1):
-                    tanh((i - 1) * QUAD + j)
-                if live(i - 2):
-                    for u in range(j * banks_a_tile, (j + 1) * banks_a_tile):
-                        turn_and_scale(i - 2, u)
-                if live(i + 2) and j < early:
-                    turn_h0((i + 2) * QUAD + j)
-                    group_h0((i + 2) * QUAD + j, nc.scalar.copy)
-            if live(i - 1):
-                for n in range((i - 1) * QUAD, i * QUAD):
-                    mish_and_statistics(n)
-                    if n > (i - 1) * QUAD:
-                        normalise(n - 1)
+        def turn(n):
+            if live(n):
+                turn_h0(n)
+
+        def group(n, copy):
+            if live(n):
+                group_h0(n, copy)
+
+        pack_h0(2)
+        pack_h0(3)
+        turn(6)
+        turn(7)
+        first_layer(0)
+        for n in range(0, GROUP):
+            add_bias(n)
+            exponential(n)
+            first_layer(n + 1)
+            pack_h0(n + 4)
+            group(n + 6, nc.scalar.copy)
+            turn(n + 8)
+        for n in range(GROUP):
+            softplus(n)
+        for n in range(GROUP, GROUP + LEAD):
+            add_bias(n)
+            first_layer(n + 1)
+            pack_h0(n + 4)
+            group(n + 6, nc.vector.tensor_copy)
+            if n + 8 < GROUP + LEAD + 7:
+                turn(n + 8)
+
+        activations = []
+        for first in range(0, TILES, GROUP):
+            for n in range(first, first + GROUP):
+                activations.append((tanh, n))
+                if live(n + GROUP):
+                    activations.append((exponential, n + GROUP))
+            for n in range(first + GROUP, first + 2 * GROUP):
+                if live(n):
+                    activations.append((softplus, n))
+
+        units = [range(n, n + QUAD) for n in range(0, TILES - QUAD, QUAD)]
+        units += [range(TILES - QUAD, TILES - 2), range(TILES - 2, TILES)]
+        starts = [unit[-1] + 3 for unit in units]
+
+        def banks_of(i):
+            return [
+                (unit, 2 * (i - start) + b)
+                for unit, start in zip(units, starts)
+                for b in range(2)
+                if 0 <= i - start < len(unit)
+            ]
+
+        for i in range(starts[-1] + len(units[-1]) + 3):
+            a = i + GROUP + LEAD
+            share = 3 if live(i + GROUP) else 1
+            now, activations = activations[:share], activations[share:]
+            banks = banks_of(i)
+            for unit, start in zip(units, starts):
+                if i == start - 2:
+                    load_base(unit)
+                if i == start + 1:
+                    copy_base(unit)
+            for k in range(max(len(now), len(banks))):
+                if k < len(now):
+                    stage, n = now[k]
+                    stage(n)
+                if k < len(banks):
+                    scale_act(*banks[k])
+                if k == 0:
+                    group(a + 6, nc.scalar.copy)
+            if live(a):
+                add_bias(a)
             if live(i):
-                for n in range(i * QUAD, (i + 1) * QUAD):
-                    exponential(n)
-                for n in range(i * QUAD, (i + 1) * QUAD):
-                    softplus(n)
-            if live(i + 1):
-                for j in range(ahead):
-                    first_layer((i + 1) * QUAD + j)
-            if live(i + 2) and early < QUAD:
-                turn_h0((i + 2) * QUAD + early)
-            if live(i - 2):
-                corrector_base(i - 2)
-                group_h1(i - 2, 0)
+                mish(i)
             if live(i - 1):
-                normalise(i * QUAD - 1)
-            if live(i - 2):
-                group_h1(i - 2, 1)
-                pack_h1(i - 2)
-                second_layer(i - 2)
-            for j in range(QUAD):
-                if live(i + 1):
-                    add_bias((i + 1) * QUAD + j)
-                    if j + ahead < QUAD:
-                        first_layer((i + 1) * QUAD + j + ahead)
-                if live(i + 2) and j >= early:
-                    group_h0((i + 2) * QUAD + j, nc.vector.tensor_copy)
-                    if j + 1 < QUAD:
-                        turn_h0((i + 2) * QUAD + j + 1)
-            if live(i + 2):
-                for n in range((i + 2) * QUAD, (i + 3) * QUAD):
-                    pack_h0(n)
-            if live(i - 2):
-                corrector(i - 2)
+                normalise(i - 1)
+            if live(a + 1):
+                first_layer(a + 1)
+            turn(a + 7)
+            for unit, bank in banks_of(i + 1):
+                turn_act(unit, bank)
+            if live(i):
+                partial_statistics(i)
+            if live(a + 4):
+                pack_h0(a + 4)
+            for unit, start in zip(units, starts):
+                if i == start:
+                    add_base(unit)
+                if i == start + len(unit) // 2 + 1:
+                    pack_h1(unit, 0)
+                if i == start + len(unit) + 1:
+                    pack_h1(unit, 1)
+                    second_layer(unit)
+                if i == start + len(unit) // 2:
+                    group_h1(unit, 0)
+                if i == start + len(unit):
+                    group_h1(unit, 1)
+                if i == start + len(unit) + 2:
+                    corrector(unit)
+            if live(i):
+                statistics(i)

@@ -54,6 +54,10 @@ def tile_actorflowode_pb_t_kernel(tc, h0, z, k1, W1, b1, ln1_g, ln1_b, W2, b2, o
         psum = ctx.enter_context(tc.psum_pool(name="psum", bufs=1))
 
         LEAD = 4
+        total, minus_mean, squares = {}, {}, {}
+        def squares_on_scalar(n):
+            return n >= TILES - GROUP and n % QUAD != QUAD - 1
+
         state, act_turned, base_bank = {}, {}, {}
         h0_sb, h0_turned, h0_grouped, h0_codes, h0_scales = {}, {}, {}, {}, {}
         sums, pre, act, partial, stats, rstd = {}, {}, {}, {}, {}, {}
@@ -78,8 +82,6 @@ def tile_actorflowode_pb_t_kernel(tc, h0, z, k1, W1, b1, ln1_g, ln1_b, W2, b2, o
         gain_rows = keep.tile([P, PASSES, PACK], BF16, name="gain_rows")
         shift_rows = keep.tile([P, PASSES, PACK], BF16, name="shift_rows")
 
-        nc.scalar.dma_start(out=bias_row[0:1, 0:HID], in_=b1.unsqueeze(0))
-        nc.scalar.dma_start(out=bias_row[0:1, HID : HID + OUT], in_=b2.unsqueeze(0))
         for rows, vector in ((gain_rows, ln1_g), (shift_rows, ln1_b)):
             nc.scalar.dma_start(out=rows[:], in_=vector.rearrange("(g p t) -> p g t", p=P, t=PACK))
 
@@ -146,7 +148,19 @@ def tile_actorflowode_pb_t_kernel(tc, h0, z, k1, W1, b1, ln1_g, ln1_b, W2, b2, o
             nc.scalar.activation(out=act[n][:], in_=act[n][:], func=FUNC.Tanh)
 
         def mish(n):
-            nc.vector.tensor_tensor(out=act[n][:], in0=pre[n][:], in1=act[n][:], op=ALU.mult)
+            if not squares_on_scalar(n):
+                nc.vector.tensor_tensor(out=act[n][:], in0=pre[n][:], in1=act[n][:], op=ALU.mult)
+                return
+            total[n] = work.tile([P, 1], F32, name="total", bufs=4)
+            nc.vector.scalar_tensor_tensor(
+                out=act[n][:], in0=pre[n][:], scalar=1.0, in1=act[n][:],
+                op0=ALU.mult, op1=ALU.mult, accum_out=total[n][:],
+            )
+            minus_mean[n] = work.tile([P, 1], F32, name="minus_mean", bufs=4)
+            nc.gpsimd.tensor_scalar(
+                out=minus_mean[n][:], in0=total[n][:], scalar1=-1.0 / HID, scalar2=0.0,
+                op0=ALU.mult, op1=ALU.add,
+            )
 
         def partial_statistics(n):
             partial[n] = work.tile([P, HALVES, 6], F32, name="partial", bufs=4)
@@ -155,21 +169,36 @@ def tile_actorflowode_pb_t_kernel(tc, h0, z, k1, W1, b1, ln1_g, ln1_b, W2, b2, o
                     out=partial[n][:, h, :], in_=act[n][:, h * BANK : (h + 1) * BANK]
                 )
 
-        def statistics(n):
-            stats[n] = work.tile([P, 2], F32, name="stats", bufs=4)
-            nc.vector.bn_aggr(out=stats[n][:], in_=partial[n][:].rearrange("p h s -> p (h s)"))
+        def one_over_root(n, variance, factor):
             shifted = work.tile([P, 1], F32, name="shifted", bufs=4)
             nc.gpsimd.tensor_scalar(
-                out=shifted[:], in0=stats[n][:, 1:2], scalar1=LN_EPS, scalar2=1.0,
-                op0=ALU.add, op1=ALU.mult,
+                out=shifted[:], in0=variance, scalar1=factor, scalar2=LN_EPS,
+                op0=ALU.mult, op1=ALU.add,
             )
             rstd[n] = work.tile([P, 1], F32, name="rstd", bufs=4)
             nc.gpsimd.tensor_tensor(out=rstd[n][:], in0=shifted[:], in1=minus_half[:], op=ALU.pow)
 
+        def statistics(n):
+            stats[n] = work.tile([P, 2], F32, name="stats", bufs=4)
+            nc.vector.bn_aggr(out=stats[n][:], in_=partial[n][:].rearrange("p h s -> p (h s)"))
+            one_over_root(n, stats[n][:, 1:2], 1.0)
+
+        def statistics_on_scalar(n):
+            squares[n] = work.tile([P, 1], F32, name="squares", bufs=4)
+            nc.scalar.activation(
+                out=pre[n][:], in_=act[n][:], func=FUNC.Square, bias=minus_mean[n][:],
+                accum_out=squares[n][:],
+            )
+            one_over_root(n, squares[n][:], 1.0 / HID)
+
         def normalise(n):
+            if squares_on_scalar(n):
+                shift, op = minus_mean[n][:], ALU.add
+            else:
+                shift, op = stats[n][:, 0:1], ALU.subtract
             nc.vector.tensor_scalar(
-                out=act[n][:], in0=act[n][:], scalar1=stats[n][:, 0:1], scalar2=rstd[n][:],
-                op0=ALU.subtract, op1=ALU.mult,
+                out=act[n][:], in0=act[n][:], scalar1=shift, scalar2=rstd[n][:],
+                op0=op, op1=ALU.mult,
             )
 
         def turn_act(unit, bank):
@@ -181,20 +210,25 @@ def tile_actorflowode_pb_t_kernel(tc, h0, z, k1, W1, b1, ln1_g, ln1_b, W2, b2, o
                 for j, n in enumerate(unit):
                     nc.tensor.transpose(turned[:, b, j, :], act[n][:, u * P : (u + 1) * P], ident[:])
 
-        def scale_act(unit, bank):
+        def scale_act(unit, bank, on_vector):
             width = len(unit) * P
             blocks = BANK // width
             if bank * blocks % PACK == 0:
                 h1[unit, bank * blocks // PACK] = work.tile([P, PACK, width], BF16, name="h1", bufs=3)
             for b in range(blocks):
                 u = bank * blocks + b
-                nc.scalar.activation(
-                    out=h1[unit, u // PACK][:, u % PACK, :],
-                    in_=act_turned[unit, bank][:, b, :, :].rearrange("p j r -> p (j r)"),
-                    func=FUNC.Identity,
-                    scale=gains[:, u : u + 1],
-                    bias=gains[:, U_TILES + u : U_TILES + u + 1],
-                )
+                turned = act_turned[unit, bank][:, b, :, :].rearrange("p j r -> p (j r)")
+                gain, shift = gains[:, u : u + 1], gains[:, U_TILES + u : U_TILES + u + 1]
+                if on_vector:
+                    nc.vector.tensor_scalar(
+                        out=h1[unit, u // PACK][:, u % PACK, :], in0=turned,
+                        scalar1=gain, scalar2=shift, op0=ALU.mult, op1=ALU.add,
+                    )
+                else:
+                    nc.scalar.activation(
+                        out=h1[unit, u // PACK][:, u % PACK, :], in_=turned,
+                        func=FUNC.Identity, scale=gain, bias=shift,
+                    )
 
         def group_h1(unit, g):
             h1_grouped[unit, g] = work.tile(
@@ -280,15 +314,16 @@ def tile_actorflowode_pb_t_kernel(tc, h0, z, k1, W1, b1, ln1_g, ln1_b, W2, b2, o
                     out=w1_raw[g][:],
                     in_=W1[g * K_PASS : (g + 1) * K_PASS, :].rearrange("(p t) c -> p t c", t=PACK),
                 )
-            w2_raw = prep.tile([P, PASSES, PACK, OUT], BF16, name="w2_raw")
+                if g == 0:
+                    nc.sync.dma_start(out=bias_row[0:1, 0:HID], in_=b1.unsqueeze(0))
+                    nc.sync.dma_start(out=bias_row[0:1, HID : HID + OUT], in_=b2.unsqueeze(0))
+            w2_raw = keep.tile([P, PASSES, PACK, OUT], BF16, name="w2_raw")
             nc.scalar.dma_start(
                 out=w2_raw[:], in_=W2.rearrange("(g p t) c -> p g t c", p=P, t=PACK)
             )
             for first in range(0, LOADS * LOAD, LOAD):
                 load_h0(first, LOAD)
 
-            nc.vector.tensor_scalar_mul(quarter[:], ident_bf16[:], STEP)
-            nc.vector.memset(quarter_ones[:], STEP)
             for h in range(HALVES):
                 cols = slice(h * BANK, (h + 1) * BANK)
                 spread = psum.tile([P, BANK], F32, name="acc", bufs=ACC)
@@ -297,6 +332,50 @@ def tile_actorflowode_pb_t_kernel(tc, h0, z, k1, W1, b1, ln1_g, ln1_b, W2, b2, o
                     out=b1_all[:, cols].rearrange("p (t m) -> p t m", t=PACK),
                     in_=spread[:].rearrange("p (m t) -> p t m", t=PACK),
                 )
+
+            w1_grouped = {}
+            for g in range(PASSES):
+                for h in range(HALVES):
+                    w1_grouped[g, h] = prep.tile(
+                        [P, BANK, PACK], BF16, name="w1_grouped", bufs=PASSES * HALVES, align_bytes=64
+                    )
+                    copy = nc.scalar.copy if (g, h) == (PASSES - 1, HALVES - 1) else nc.vector.tensor_copy
+                    copy(
+                        out=w1_grouped[g, h][:].rearrange("p (t m) j -> p t m j", t=PACK),
+                        in_=w1_raw[g][:, :, h * BANK : (h + 1) * BANK].rearrange(
+                            "p j (m t) -> p t m j", t=PACK
+                        ),
+                    )
+
+            for n in range(2):
+                turn_h0(n)
+                group_h0(n, nc.vector.tensor_copy)
+            for n in range(2, 6):
+                turn_h0(n)
+                group_h0(n, nc.scalar.copy)
+            turn_h0(6)
+            turn_h0(7)
+            for h in range(HALVES):
+                cols = slice(h * BANK, (h + 1) * BANK)
+                for g in range(PASSES):
+                    nc.vector.quantize_mx(
+                        out=w1_codes[:, g, cols].bitcast(FP8X4),
+                        scales=w1_scales[:, g, cols],
+                        in_=w1_grouped[g, h][:].rearrange("p c t -> p (c t)"),
+                    )
+                pack_h0(h)
+
+        def prepare_w2():
+            w2_grouped = work.tile([P, PASSES, OUT, PACK], BF16, name="w2_grouped", align_bytes=64)
+            for g in range(PASSES):
+                interleave_four(nc.vector.tensor_copy, w2_grouped[:, g, :, :], w2_raw[:, g, :, :])
+            nc.vector.quantize_mx(
+                out=w2_codes[:].rearrange("p g c -> p (g c)").bitcast(FP8X4),
+                scales=w2_scales[:].rearrange("p g c -> p (g c)"),
+                in_=w2_grouped[:].rearrange("p g c t -> p (g c t)"),
+            )
+            nc.vector.tensor_scalar_mul(quarter[:], ident_bf16[:], STEP)
+            nc.vector.memset(quarter_ones[:], STEP)
             for j in range(QUAD):
                 nc.vector.tensor_copy(
                     out=b2_rows[:, j * OUT : (j + 1) * OUT], in_=bias_row[:, HID : HID + OUT]
@@ -306,44 +385,6 @@ def tile_actorflowode_pb_t_kernel(tc, h0, z, k1, W1, b1, ln1_g, ln1_b, W2, b2, o
                     out=gains[:, v * U_TILES : (v + 1) * U_TILES],
                     in_=rows[:].rearrange("p g t -> p (g t)"),
                 )
-
-            turn_h0(0)
-            turn_h0(1)
-            w1_grouped = {}
-            w2_grouped = prep.tile([P, PASSES, OUT, PACK], BF16, name="w2_grouped", align_bytes=64)
-            for g in range(PASSES):
-                for h in range(HALVES):
-                    w1_grouped[g, h] = prep.tile(
-                        [P, BANK, PACK], BF16, name="w1_grouped", bufs=PASSES * HALVES, align_bytes=64
-                    )
-                    copy = nc.vector.tensor_copy if h == 0 else nc.scalar.copy
-                    copy(
-                        out=w1_grouped[g, h][:].rearrange("p (t m) j -> p t m j", t=PACK),
-                        in_=w1_raw[g][:, :, h * BANK : (h + 1) * BANK].rearrange(
-                            "p j (m t) -> p t m j", t=PACK
-                        ),
-                    )
-            for n in range(2):
-                group_h0(n, nc.vector.tensor_copy)
-            for n in range(2, 6):
-                turn_h0(n)
-                group_h0(n, nc.scalar.copy)
-            for h in range(HALVES):
-                for g in range(PASSES):
-                    cols = slice(h * BANK, (h + 1) * BANK)
-                    nc.vector.quantize_mx(
-                        out=w1_codes[:, g, cols].bitcast(FP8X4),
-                        scales=w1_scales[:, g, cols],
-                        in_=w1_grouped[g, h][:].rearrange("p c t -> p (c t)"),
-                    )
-                pack_h0(h)
-            for g in range(PASSES):
-                interleave_four(nc.vector.tensor_copy, w2_grouped[:, g, :, :], w2_raw[:, g, :, :])
-            nc.vector.quantize_mx(
-                out=w2_codes[:].rearrange("p g c -> p (g c)").bitcast(FP8X4),
-                scales=w2_scales[:].rearrange("p g c -> p (g c)"),
-                in_=w2_grouped[:].rearrange("p g c t -> p (g c t)"),
-            )
         work = ctx.enter_context(tc.tile_pool(name="work", bufs=1))
 
         def live(n):
@@ -357,27 +398,50 @@ def tile_actorflowode_pb_t_kernel(tc, h0, z, k1, W1, b1, ln1_g, ln1_b, W2, b2, o
             if live(n):
                 group_h0(n, copy)
 
-        pack_h0(2)
-        pack_h0(3)
-        turn(6)
-        turn(7)
+
+        def live(n):
+            return 0 <= n < TILES
+
+        def turn(n):
+            if live(n):
+                turn_h0(n)
+
+        def group(n, copy):
+            if live(n):
+                group_h0(n, copy)
+
+        def pack(n):
+            if live(n):
+                pack_h0(n)
+
+        def multiply(n):
+            if live(n):
+                first_layer(n)
+
         first_layer(0)
-        for n in range(0, GROUP):
+        for n in range(GROUP):
             add_bias(n)
             exponential(n)
-            first_layer(n + 1)
-            pack_h0(n + 4)
-            group(n + 6, nc.scalar.copy)
-            turn(n + 8)
+            if n + 1 < GROUP:
+                first_layer(n + 1)
+            if n + 2 < GROUP:
+                pack_h0(n + 2)
+            if n + 6 < GROUP:
+                group_h0(n + 6, nc.scalar.copy)
         for n in range(GROUP):
             softplus(n)
-        for n in range(GROUP, GROUP + LEAD):
-            add_bias(n)
-            first_layer(n + 1)
-            pack_h0(n + 4)
-            group(n + 6, nc.vector.tensor_copy)
-            if n + 8 < GROUP + LEAD + 7:
-                turn(n + 8)
+        prepare_w2()
+        added = GROUP + LEAD
+        for k in range(GROUP, added + 4):
+            turn(k)
+            if k - 4 >= GROUP:
+                add_bias(k - 4)
+            if GROUP <= k - 1 < added + 3:
+                group(k - 1, nc.vector.tensor_copy)
+            if k - 3 >= GROUP:
+                multiply(k - 3)
+            if GROUP <= k - 2 < added + 2:
+                pack(k - 2)
 
         activations = []
         for first in range(0, TILES, GROUP):
@@ -391,7 +455,7 @@ def tile_actorflowode_pb_t_kernel(tc, h0, z, k1, W1, b1, ln1_g, ln1_b, W2, b2, o
 
         units = [range(n, n + QUAD) for n in range(0, TILES - QUAD, QUAD)]
         units += [range(TILES - QUAD, TILES - 2), range(TILES - 2, TILES)]
-        starts = [unit[-1] + 3 for unit in units]
+        starts = [unit[-1] + (4 if squares_on_scalar(unit[-1]) else 3) for unit in units]
 
         def banks_of(i):
             return [
@@ -402,10 +466,11 @@ def tile_actorflowode_pb_t_kernel(tc, h0, z, k1, W1, b1, ln1_g, ln1_b, W2, b2, o
             ]
 
         for i in range(starts[-1] + len(units[-1]) + 3):
-            a = i + GROUP + LEAD
+            a = i + added
             share = 3 if live(i + GROUP) else 1
             now, activations = activations[:share], activations[share:]
             banks = banks_of(i)
+            vector_helps = not live(a) and live(i + GROUP)
             for unit, start in zip(units, starts):
                 if i == start - 2:
                     load_base(unit)
@@ -415,25 +480,22 @@ def tile_actorflowode_pb_t_kernel(tc, h0, z, k1, W1, b1, ln1_g, ln1_b, W2, b2, o
                 if k < len(now):
                     stage, n = now[k]
                     stage(n)
-                if k < len(banks):
-                    scale_act(*banks[k])
+                if k == min(1, len(now)) and live(i - 1) and squares_on_scalar(i - 1):
+                    statistics_on_scalar(i - 1)
+                if k < len(banks) and not (vector_helps and k % 2 == 1):
+                    scale_act(*banks[k], False)
                 if k == 0:
-                    group(a + 6, nc.scalar.copy)
+                    group(a + 3, nc.vector.tensor_copy if (a + 3) % 4 == 3 else nc.scalar.copy)
             if live(a):
                 add_bias(a)
+            multiply(a + 1)
+            turn(a + 4)
             if live(i):
                 mish(i)
-            if live(i - 1):
-                normalise(i - 1)
-            if live(a + 1):
-                first_layer(a + 1)
-            turn(a + 7)
-            for unit, bank in banks_of(i + 1):
-                turn_act(unit, bank)
-            if live(i):
-                partial_statistics(i)
-            if live(a + 4):
-                pack_h0(a + 4)
+            if vector_helps:
+                for unit, bank in banks[1::2]:
+                    scale_act(unit, bank, True)
+            pack(a + 2)
             for unit, start in zip(units, starts):
                 if i == start:
                     add_base(unit)
@@ -448,5 +510,13 @@ def tile_actorflowode_pb_t_kernel(tc, h0, z, k1, W1, b1, ln1_g, ln1_b, W2, b2, o
                     group_h1(unit, 1)
                 if i == start + len(unit) + 2:
                     corrector(unit)
-            if live(i):
+            if live(i) and not squares_on_scalar(i):
+                partial_statistics(i)
+            if live(i - 2) and squares_on_scalar(i - 2):
+                normalise(i - 2)
+            if live(i - 1) and not squares_on_scalar(i - 1):
+                normalise(i - 1)
+            if live(i) and not squares_on_scalar(i):
                 statistics(i)
+            for unit, bank in banks_of(i + 1):
+                turn_act(unit, bank)

@@ -51,6 +51,7 @@ def tile_actorflowode_pb_t_kernel(tc, h0, z, k1, W1, b1, ln1_g, ln1_b, W2, b2, o
         ctx.enter_context(tc.manual_schedule())
         keep = ctx.enter_context(tc.tile_pool(name="keep", bufs=1))
         feed = ctx.enter_context(tc.tile_pool(name="feed", bufs=1))
+        wide = ctx.enter_context(tc.tile_pool(name="wide", bufs=1))
         psum = ctx.enter_context(tc.psum_pool(name="psum", bufs=1))
 
         LEAD = 4
@@ -112,8 +113,8 @@ def tile_actorflowode_pb_t_kernel(tc, h0, z, k1, W1, b1, ln1_g, ln1_b, W2, b2, o
                 out=h0_codes[n][:].bitcast(FP8X4), scales=h0_scales[n][:], in_=h0_grouped[n][:]
             )
 
-        def first_layer(n):
-            for h in range(HALVES):
+        def first_layer(n, halves=range(HALVES)):
+            for h in halves:
                 cols = slice(h * BANK, (h + 1) * BANK)
                 acc = psum.tile([P, BANK], F32, name="acc", bufs=ACC)
                 sums[n, h] = acc
@@ -123,23 +124,30 @@ def tile_actorflowode_pb_t_kernel(tc, h0, z, k1, W1, b1, ln1_g, ln1_b, W2, b2, o
                         out=acc[:],
                         lhsT=h0_codes[n][:, rows].bitcast(FP8X4),
                         lhsT_scale=h0_scales[n][:, rows],
-                        rhs=w1_codes[:, g, cols].bitcast(FP8X4),
-                        rhs_scale=w1_scales[:, g, cols],
+                        rhs=w1_codes[g, h][:].bitcast(FP8X4),
+                        rhs_scale=w1_scales[g, h][:],
                         start=(g == 0),
                         stop=(g == PASSES - 1),
                     )
 
-        def add_bias(n):
-            pre[n] = work.tile([P, HID], F32, name="pre", bufs=13)
-            for h in range(HALVES):
+        def add_bias(n, halves=range(HALVES)):
+            for h in halves:
+                if h == 0:
+                    pre[n] = wide.tile([P, HID], F32, name="pre", bufs=13)
                 cols = slice(h * BANK, (h + 1) * BANK)
                 nc.vector.tensor_tensor(
                     out=pre[n][:, cols], in0=sums[n, h][:], in1=b1_all[:, cols], op=ALU.add
                 )
 
         def exponential(n):
-            act[n] = work.tile([P, HID], F32, name="act", bufs=22)
+            act[n] = wide.tile([P, HID], F32, name="act", bufs=22)
             nc.scalar.activation(out=act[n][:], in_=pre[n][:], func=FUNC.Exp)
+
+        def exponential_half(n, h):
+            if h == 0:
+                act[n] = wide.tile([P, HID], F32, name="act", bufs=22)
+            cols = slice(h * BANK, (h + 1) * BANK)
+            nc.scalar.activation(out=act[n][:, cols], in_=pre[n][:, cols], func=FUNC.Exp)
 
         def softplus(n):
             nc.scalar.activation(out=act[n][:], in_=act[n][:], func=FUNC.Ln, bias=1.0)
@@ -296,8 +304,7 @@ def tile_actorflowode_pb_t_kernel(tc, h0, z, k1, W1, b1, ln1_g, ln1_b, W2, b2, o
             )
             nc.sync.dma_start(out=out_rows[:, unit[0] : unit[-1] + 1, :], in_=result[:])
 
-        w1_codes = keep.tile([P, PASSES, HID], U32, name="w1_codes", align_bytes=64)
-        w1_scales = keep.tile([P, PASSES, HID], U8, name="w1_scales", align_bytes=64)
+        w1_codes, w1_scales = {}, {}
         w2_codes = keep.tile([P, PASSES, OUT], U32, name="w2_codes", align_bytes=64)
         w2_scales = keep.tile([P, PASSES, OUT], U8, name="w2_scales", align_bytes=64)
         b1_all = keep.tile([P, HID], F32, name="b1_all")
@@ -308,20 +315,26 @@ def tile_actorflowode_pb_t_kernel(tc, h0, z, k1, W1, b1, ln1_g, ln1_b, W2, b2, o
 
         with tc.tile_pool(name="prep", bufs=1) as prep:
             w1_raw = {}
-            for g in range(PASSES):
-                w1_raw[g] = prep.tile([P, PACK, HID], BF16, name="w1_raw", bufs=PASSES)
-                nc.sync.dma_start(
-                    out=w1_raw[g][:],
-                    in_=W1[g * K_PASS : (g + 1) * K_PASS, :].rearrange("(p t) c -> p t c", t=PACK),
-                )
-                if g == 0:
-                    nc.sync.dma_start(out=bias_row[0:1, 0:HID], in_=b1.unsqueeze(0))
-                    nc.sync.dma_start(out=bias_row[0:1, HID : HID + OUT], in_=b2.unsqueeze(0))
+
+            def load_w1(h):
+                cols = slice(h * BANK, (h + 1) * BANK)
+                for g in range(PASSES):
+                    w1_raw[g, h] = prep.tile([P, PACK, BANK], BF16, name="w1_raw", bufs=PASSES * HALVES)
+                    nc.sync.dma_start(
+                        out=w1_raw[g, h][:],
+                        in_=W1[g * K_PASS : (g + 1) * K_PASS, cols].rearrange("(p t) c -> p t c", t=PACK),
+                    )
+
+            load_w1(0)
+            nc.sync.dma_start(out=bias_row[0:1, 0:HID], in_=b1.unsqueeze(0))
+            nc.sync.dma_start(out=bias_row[0:1, HID : HID + OUT], in_=b2.unsqueeze(0))
+            load_h0(0, LOAD)
+            load_w1(1)
             w2_raw = keep.tile([P, PASSES, PACK, OUT], BF16, name="w2_raw")
             nc.scalar.dma_start(
                 out=w2_raw[:], in_=W2.rearrange("(g p t) c -> p g t c", p=P, t=PACK)
             )
-            for first in range(0, LOADS * LOAD, LOAD):
+            for first in range(LOAD, LOADS * LOAD, LOAD):
                 load_h0(first, LOAD)
 
             for h in range(HALVES):
@@ -334,36 +347,45 @@ def tile_actorflowode_pb_t_kernel(tc, h0, z, k1, W1, b1, ln1_g, ln1_b, W2, b2, o
                 )
 
             w1_grouped = {}
-            for g in range(PASSES):
-                for h in range(HALVES):
-                    w1_grouped[g, h] = prep.tile(
-                        [P, BANK, PACK], BF16, name="w1_grouped", bufs=PASSES * HALVES, align_bytes=64
-                    )
-                    copy = nc.scalar.copy if (g, h) == (PASSES - 1, HALVES - 1) else nc.vector.tensor_copy
-                    copy(
-                        out=w1_grouped[g, h][:].rearrange("p (t m) j -> p t m j", t=PACK),
-                        in_=w1_raw[g][:, :, h * BANK : (h + 1) * BANK].rearrange(
-                            "p j (m t) -> p t m j", t=PACK
-                        ),
-                    )
 
+            def regroup_w1(g, h, copy):
+                w1_grouped[g, h] = prep.tile(
+                    [P, BANK, PACK], BF16, name="w1_grouped", bufs=PASSES * HALVES, align_bytes=64
+                )
+                copy(
+                    out=w1_grouped[g, h][:].rearrange("p (t m) j -> p t m j", t=PACK),
+                    in_=w1_raw[g, h][:].rearrange("p j (m t) -> p t m j", t=PACK),
+                )
+
+            def pack_w1(g, h):
+                w1_codes[g, h] = keep.tile([P, BANK], U32, name="w1_codes", bufs=4, align_bytes=64)
+                w1_scales[g, h] = keep.tile([P, BANK], U8, name="w1_scales", bufs=4, align_bytes=64)
+                nc.vector.quantize_mx(
+                    out=w1_codes[g, h][:].bitcast(FP8X4), scales=w1_scales[g, h][:],
+                    in_=w1_grouped[g, h][:].rearrange("p c t -> p (c t)"),
+                )
+
+            for g in range(PASSES):
+                regroup_w1(g, 0, nc.vector.tensor_copy)
             for n in range(2):
                 turn_h0(n)
-                group_h0(n, nc.vector.tensor_copy)
+                group_h0(n, nc.scalar.copy)
+            for g in range(PASSES):
+                pack_w1(g, 0)
+            for n in range(2):
+                pack_h0(n)
+                first_layer(n, [0])
+            regroup_w1(0, 1, nc.scalar.copy)
+            add_bias(0, [0])
+            regroup_w1(1, 1, nc.vector.tensor_copy)
+            add_bias(1, [0])
             for n in range(2, 6):
                 turn_h0(n)
                 group_h0(n, nc.scalar.copy)
             turn_h0(6)
             turn_h0(7)
-            for h in range(HALVES):
-                cols = slice(h * BANK, (h + 1) * BANK)
-                for g in range(PASSES):
-                    nc.vector.quantize_mx(
-                        out=w1_codes[:, g, cols].bitcast(FP8X4),
-                        scales=w1_scales[:, g, cols],
-                        in_=w1_grouped[g, h][:].rearrange("p c t -> p (c t)"),
-                    )
-                pack_h0(h)
+            for g in range(PASSES):
+                pack_w1(g, 1)
 
         def prepare_w2():
             w2_grouped = work.tile([P, PASSES, OUT, PACK], BF16, name="w2_grouped", align_bytes=64)
@@ -418,12 +440,19 @@ def tile_actorflowode_pb_t_kernel(tc, h0, z, k1, W1, b1, ln1_g, ln1_b, W2, b2, o
             if live(n):
                 first_layer(n)
 
-        first_layer(0)
         for n in range(GROUP):
-            add_bias(n)
-            exponential(n)
+            if n < 2:
+                if n == 0:
+                    exponential_half(0, 0)
+                    exponential_half(1, 0)
+                    first_layer(0, [1])
+                add_bias(n, [1])
+                exponential_half(n, 1)
+            else:
+                add_bias(n)
+                exponential(n)
             if n + 1 < GROUP:
-                first_layer(n + 1)
+                first_layer(n + 1, range(HALVES) if n > 0 else [1])
             if n + 2 < GROUP:
                 pack_h0(n + 2)
             if n + 6 < GROUP:

@@ -24,7 +24,7 @@ HALVES = HID // BANK
 LOAD = 2
 ACC = 3
 TURNED = 4
-LOADS = 4
+LOADS = 3
 GROUP = 8
 U_TILES = HID // P
 LN_EPS = 1e-5
@@ -56,6 +56,11 @@ def tile_actorflowode_pb_t_kernel(tc, h0, z, k1, W1, b1, ln1_g, ln1_b, W2, b2, o
 
         LEAD = 4
         total, minus_mean, squares = {}, {}, {}
+        value = {}
+
+        def on_gpsimd(n):
+            return n < TILES - GROUP - LEAD
+
         def squares_on_scalar(n):
             return n >= TILES - GROUP and n % QUAD != QUAD - 1
 
@@ -140,12 +145,12 @@ def tile_actorflowode_pb_t_kernel(tc, h0, z, k1, W1, b1, ln1_g, ln1_b, W2, b2, o
                 )
 
         def exponential(n):
-            act[n] = wide.tile([P, HID], F32, name="act", bufs=22)
+            act[n] = wide.tile([P, HID], F32, name="act", bufs=21)
             nc.scalar.activation(out=act[n][:], in_=pre[n][:], func=FUNC.Exp)
 
         def exponential_half(n, h):
             if h == 0:
-                act[n] = wide.tile([P, HID], F32, name="act", bufs=22)
+                act[n] = wide.tile([P, HID], F32, name="act", bufs=21)
             cols = slice(h * BANK, (h + 1) * BANK)
             nc.scalar.activation(out=act[n][:, cols], in_=pre[n][:, cols], func=FUNC.Exp)
 
@@ -156,6 +161,11 @@ def tile_actorflowode_pb_t_kernel(tc, h0, z, k1, W1, b1, ln1_g, ln1_b, W2, b2, o
             nc.scalar.activation(out=act[n][:], in_=act[n][:], func=FUNC.Tanh)
 
         def mish(n):
+            if on_gpsimd(n):
+                value[n] = wide.tile([P, HID], F32, name="value", bufs=2)
+                nc.gpsimd.tensor_tensor(out=value[n][:], in0=pre[n][:], in1=act[n][:], op=ALU.mult)
+                return
+            value[n] = act[n]
             if not squares_on_scalar(n):
                 nc.vector.tensor_tensor(out=act[n][:], in0=pre[n][:], in1=act[n][:], op=ALU.mult)
                 return
@@ -174,7 +184,7 @@ def tile_actorflowode_pb_t_kernel(tc, h0, z, k1, W1, b1, ln1_g, ln1_b, W2, b2, o
             partial[n] = work.tile([P, HALVES, 6], F32, name="partial", bufs=4)
             for h in range(HALVES):
                 nc.vector.bn_stats(
-                    out=partial[n][:, h, :], in_=act[n][:, h * BANK : (h + 1) * BANK]
+                    out=partial[n][:, h, :], in_=value[n][:, h * BANK : (h + 1) * BANK]
                 )
 
         def one_over_root(n, variance, factor):
@@ -205,7 +215,7 @@ def tile_actorflowode_pb_t_kernel(tc, h0, z, k1, W1, b1, ln1_g, ln1_b, W2, b2, o
             else:
                 shift, op = stats[n][:, 0:1], ALU.subtract
             nc.vector.tensor_scalar(
-                out=act[n][:], in0=act[n][:], scalar1=shift, scalar2=rstd[n][:],
+                out=act[n][:], in0=value[n][:], scalar1=shift, scalar2=rstd[n][:],
                 op0=op, op1=ALU.mult,
             )
 
@@ -513,20 +523,33 @@ def tile_actorflowode_pb_t_kernel(tc, h0, z, k1, W1, b1, ln1_g, ln1_b, W2, b2, o
                     statistics_on_scalar(i - 1)
                 if k < len(banks) and not (vector_helps and k % 2 == 1):
                     scale_act(*banks[k], False)
-                if k == 0:
-                    group(a + 3, nc.vector.tensor_copy if (a + 3) % 4 == 3 else nc.scalar.copy)
+            if live(i - 2) and on_gpsimd(i - 2):
+                normalise(i - 2)
+            early = live(a)
+            if early:
+                for unit, bank in banks_of(i + 1):
+                    turn_act(unit, bank)
+                for unit, start in zip(units, starts):
+                    if i == start:
+                        add_base(unit)
+            if live(i) and on_gpsimd(i):
+                mish(i)
+            if live(i - 1) and on_gpsimd(i - 1):
+                partial_statistics(i - 1)
+                statistics(i - 1)
             if live(a):
                 add_bias(a)
+            group(a + 3, nc.vector.tensor_copy)
             multiply(a + 1)
             turn(a + 4)
-            if live(i):
+            if live(i) and not on_gpsimd(i):
                 mish(i)
             if vector_helps:
                 for unit, bank in banks[1::2]:
                     scale_act(unit, bank, True)
             pack(a + 2)
             for unit, start in zip(units, starts):
-                if i == start:
+                if i == start and not early:
                     add_base(unit)
                 if i == start + len(unit) // 2 + 1:
                     pack_h1(unit, 0)
@@ -539,13 +562,14 @@ def tile_actorflowode_pb_t_kernel(tc, h0, z, k1, W1, b1, ln1_g, ln1_b, W2, b2, o
                     group_h1(unit, 1)
                 if i == start + len(unit) + 2:
                     corrector(unit)
-            if live(i) and not squares_on_scalar(i):
+            if live(i) and not squares_on_scalar(i) and not on_gpsimd(i):
                 partial_statistics(i)
             if live(i - 2) and squares_on_scalar(i - 2):
                 normalise(i - 2)
-            if live(i - 1) and not squares_on_scalar(i - 1):
+            if live(i - 1) and not squares_on_scalar(i - 1) and not on_gpsimd(i - 1):
                 normalise(i - 1)
-            if live(i) and not squares_on_scalar(i):
+            if live(i) and not squares_on_scalar(i) and not on_gpsimd(i):
                 statistics(i)
-            for unit, bank in banks_of(i + 1):
-                turn_act(unit, bank)
+            if not early:
+                for unit, bank in banks_of(i + 1):
+                    turn_act(unit, bank)

@@ -24,6 +24,7 @@ HALVES = HID // BANK
 LOAD = 2
 ACC = 3
 TURNED = 4
+GPSIMD_COLS = 768
 LOADS = 3
 GROUP = 8
 U_TILES = HID // P
@@ -163,7 +164,10 @@ def tile_actorflowode_pb_t_kernel(tc, h0, z, k1, W1, b1, ln1_g, ln1_b, W2, b2, o
         def mish(n):
             if on_gpsimd(n):
                 value[n] = wide.tile([P, HID], F32, name="value", bufs=2)
-                nc.gpsimd.tensor_tensor(out=value[n][:], in0=pre[n][:], in1=act[n][:], op=ALU.mult)
+                cols = slice(0, GPSIMD_COLS)
+                nc.gpsimd.tensor_tensor(
+                    out=value[n][:, cols], in0=pre[n][:, cols], in1=act[n][:, cols], op=ALU.mult
+                )
                 return
             value[n] = act[n]
             if not squares_on_scalar(n):
@@ -178,6 +182,12 @@ def tile_actorflowode_pb_t_kernel(tc, h0, z, k1, W1, b1, ln1_g, ln1_b, W2, b2, o
             nc.gpsimd.tensor_scalar(
                 out=minus_mean[n][:], in0=total[n][:], scalar1=-1.0 / HID, scalar2=0.0,
                 op0=ALU.mult, op1=ALU.add,
+            )
+
+        def mish_rest(n):
+            cols = slice(GPSIMD_COLS, HID)
+            nc.vector.tensor_tensor(
+                out=value[n][:, cols], in0=pre[n][:, cols], in1=act[n][:, cols], op=ALU.mult
             )
 
         def partial_statistics(n):
@@ -562,6 +572,8 @@ def tile_actorflowode_pb_t_kernel(tc, h0, z, k1, W1, b1, ln1_g, ln1_b, W2, b2, o
                     group_h1(unit, 1)
                 if i == start + len(unit) + 2:
                     corrector(unit)
+            if live(i) and on_gpsimd(i):
+                mish_rest(i)
             if live(i) and not squares_on_scalar(i) and not on_gpsimd(i):
                 partial_statistics(i)
             if live(i - 2) and squares_on_scalar(i - 2):

@@ -24,7 +24,7 @@ HALVES = HID // BANK
 LOAD = 2
 ACC = 3
 TURNED = 4
-GPSIMD_COLS = 768
+GPSIMD_COLS = 704
 LOADS = 3
 GROUP = 8
 U_TILES = HID // P
@@ -178,8 +178,10 @@ def tile_actorflowode_pb_t_kernel(tc, h0, z, k1, W1, b1, ln1_g, ln1_b, W2, b2, o
                 out=act[n][:], in0=pre[n][:], scalar=1.0, in1=act[n][:],
                 op0=ALU.mult, op1=ALU.mult, accum_out=total[n][:],
             )
+
+        def find_mean(n):
             minus_mean[n] = work.tile([P, 1], F32, name="minus_mean", bufs=4)
-            nc.gpsimd.tensor_scalar(
+            nc.vector.tensor_scalar(
                 out=minus_mean[n][:], in0=total[n][:], scalar1=-1.0 / HID, scalar2=0.0,
                 op0=ALU.mult, op1=ALU.add,
             )
@@ -550,6 +552,10 @@ def tile_actorflowode_pb_t_kernel(tc, h0, z, k1, W1, b1, ln1_g, ln1_b, W2, b2, o
             if live(a):
                 add_bias(a)
             group(a + 3, nc.vector.tensor_copy)
+            if early:
+                for unit, start in zip(units, starts):
+                    if i == start + len(unit) + 2:
+                        corrector(unit)
             multiply(a + 1)
             turn(a + 4)
             if live(i) and not on_gpsimd(i):
@@ -570,8 +576,10 @@ def tile_actorflowode_pb_t_kernel(tc, h0, z, k1, W1, b1, ln1_g, ln1_b, W2, b2, o
                     group_h1(unit, 0)
                 if i == start + len(unit):
                     group_h1(unit, 1)
-                if i == start + len(unit) + 2:
+                if i == start + len(unit) + 2 and not early:
                     corrector(unit)
+            if live(i) and squares_on_scalar(i):
+                find_mean(i)
             if live(i) and on_gpsimd(i):
                 mish_rest(i)
             if live(i) and not squares_on_scalar(i) and not on_gpsimd(i):

@@ -199,27 +199,35 @@ def tile_actorflowode_pb_t_kernel(tc, h0, z, k1, W1, b1, ln1_g, ln1_b, W2, b2, o
                     out=partial[n][:, h, :], in_=value[n][:, h * BANK : (h + 1) * BANK]
                 )
 
-        def one_over_root(n, variance, factor):
-            shifted = work.tile([P, 1], F32, name="shifted", bufs=4)
-            nc.gpsimd.tensor_scalar(
-                out=shifted[:], in0=variance, scalar1=factor, scalar2=LN_EPS,
-                op0=ALU.mult, op1=ALU.add,
-            )
+        def one_over_root(n, shifted):
             rstd[n] = work.tile([P, 1], F32, name="rstd", bufs=4)
             nc.gpsimd.tensor_tensor(out=rstd[n][:], in0=shifted[:], in1=minus_half[:], op=ALU.pow)
 
-        def statistics(n):
+        def aggregate(n):
             stats[n] = work.tile([P, 2], F32, name="stats", bufs=4)
             nc.vector.bn_aggr(out=stats[n][:], in_=partial[n][:].rearrange("p h s -> p (h s)"))
-            one_over_root(n, stats[n][:, 1:2], 1.0)
 
-        def statistics_on_scalar(n):
+        def finish(n, engine):
+            shifted = work.tile([P, 1], F32, name="shifted", bufs=4)
+            engine.tensor_scalar(
+                out=shifted[:], in0=stats[n][:, 1:2], scalar1=1.0, scalar2=LN_EPS,
+                op0=ALU.mult, op1=ALU.add,
+            )
+            one_over_root(n, shifted)
+
+        def sum_squares(n):
             squares[n] = work.tile([P, 1], F32, name="squares", bufs=4)
             nc.scalar.activation(
                 out=pre[n][:], in_=act[n][:], func=FUNC.Square, bias=minus_mean[n][:],
                 accum_out=squares[n][:],
             )
-            one_over_root(n, squares[n][:], 1.0 / HID)
+
+        def finish_on_scalar(n):
+            shifted = work.tile([P, 1], F32, name="shifted_squares", bufs=4)
+            nc.scalar.activation(
+                out=shifted[:], in_=squares[n][:], func=FUNC.Identity, scale=1.0 / HID, bias=LN_EPS
+            )
+            one_over_root(n, shifted)
 
         def normalise(n):
             if squares_on_scalar(n):
@@ -532,9 +540,11 @@ def tile_actorflowode_pb_t_kernel(tc, h0, z, k1, W1, b1, ln1_g, ln1_b, W2, b2, o
                     stage, n = now[k]
                     stage(n)
                 if k == min(1, len(now)) and live(i - 1) and squares_on_scalar(i - 1):
-                    statistics_on_scalar(i - 1)
+                    sum_squares(i - 1)
                 if k < len(banks) and not (vector_helps and k % 2 == 1):
                     scale_act(*banks[k], False)
+            if live(i - 1) and squares_on_scalar(i - 1):
+                finish_on_scalar(i - 1)
             if live(i - 2) and on_gpsimd(i - 2):
                 normalise(i - 2)
             early = live(a)
@@ -548,7 +558,8 @@ def tile_actorflowode_pb_t_kernel(tc, h0, z, k1, W1, b1, ln1_g, ln1_b, W2, b2, o
                 mish(i)
             if live(i - 1) and on_gpsimd(i - 1):
                 partial_statistics(i - 1)
-                statistics(i - 1)
+                aggregate(i - 1)
+                finish(i - 1, nc.gpsimd)
             if live(a):
                 add_bias(a)
             group(a + 3, nc.vector.tensor_copy)
@@ -560,6 +571,8 @@ def tile_actorflowode_pb_t_kernel(tc, h0, z, k1, W1, b1, ln1_g, ln1_b, W2, b2, o
             turn(a + 4)
             if live(i) and not on_gpsimd(i):
                 mish(i)
+            if live(i - 1) and not squares_on_scalar(i - 1) and not on_gpsimd(i - 1):
+                finish(i - 1, nc.vector)
             if vector_helps:
                 for unit, bank in banks[1::2]:
                     scale_act(unit, bank, True)
@@ -589,7 +602,7 @@ def tile_actorflowode_pb_t_kernel(tc, h0, z, k1, W1, b1, ln1_g, ln1_b, W2, b2, o
             if live(i - 1) and not squares_on_scalar(i - 1) and not on_gpsimd(i - 1):
                 normalise(i - 1)
             if live(i) and not squares_on_scalar(i) and not on_gpsimd(i):
-                statistics(i)
+                aggregate(i)
             if not early:
                 for unit, bank in banks_of(i + 1):
                     turn_act(unit, bank)

@@ -25,6 +25,10 @@ LOAD = 2
 ACC = 3
 TURNED = 4
 GPSIMD_COLS = 704
+GPSIMD_COLS_LATE = 0
+ACTS = 22
+PRES = 14
+PAIR = 2
 LOADS = 3
 GROUP = 8
 U_TILES = HID // P
@@ -55,19 +59,31 @@ def tile_actorflowode_pb_t_kernel(tc, h0, z, k1, W1, b1, ln1_g, ln1_b, W2, b2, o
         wide = ctx.enter_context(tc.tile_pool(name="wide", bufs=1))
         psum = ctx.enter_context(tc.psum_pool(name="psum", bufs=1))
 
-        LEAD = 4
+        LEAD = 5
         total, minus_mean, squares = {}, {}, {}
         value = {}
 
         def on_gpsimd(n):
-            return n < TILES - GROUP - LEAD
+            return n < 32
+
+        def gpsimd_cols(n):
+            if squares_on_scalar(n):
+                return 0
+            return GPSIMD_COLS if live(n + added) else GPSIMD_COLS_LATE
+
+        def live(n):
+            return 0 <= n < TILES
+
+        def gpsimd_normalises(n):
+            return n < 21
 
         def squares_on_scalar(n):
-            return n >= TILES - GROUP and n % QUAD != QUAD - 1
+            return n >= 24 and n % 2 == 1
 
         state, act_turned, base_bank = {}, {}, {}
         h0_sb, h0_turned, h0_grouped, h0_codes, h0_scales = {}, {}, {}, {}, {}
         sums, pre, act, partial, stats, rstd = {}, {}, {}, {}, {}, {}
+        pair_stats, pair_shifted, pair_rstd, pair_offset = {}, {}, {}, {}
         h1, h1_grouped, h1_codes, h1_scales, head, base = {}, {}, {}, {}, {}, {}
 
         def load_h0(first, count):
@@ -82,7 +98,7 @@ def tile_actorflowode_pb_t_kernel(tc, h0, z, k1, W1, b1, ln1_g, ln1_b, W2, b2, o
         make_identity(nc, ident_bf16[:])
         ones = keep.tile([P, P], BF16, name="ones")
         nc.vector.memset(ones[:], 1.0)
-        minus_half = keep.tile([P, 1], F32, name="minus_half")
+        minus_half = keep.tile([P, PAIR], F32, name="minus_half")
         nc.vector.memset(minus_half[:], -0.5)
         bias_row = keep.tile([P, HID + OUT], BF16, name="bias_row")
         nc.vector.memset(bias_row[:], 0.0)
@@ -139,19 +155,19 @@ def tile_actorflowode_pb_t_kernel(tc, h0, z, k1, W1, b1, ln1_g, ln1_b, W2, b2, o
         def add_bias(n, halves=range(HALVES)):
             for h in halves:
                 if h == 0:
-                    pre[n] = wide.tile([P, HID], F32, name="pre", bufs=13)
+                    pre[n] = wide.tile([P, HID], F32, name="pre", bufs=PRES)
                 cols = slice(h * BANK, (h + 1) * BANK)
                 nc.vector.tensor_tensor(
                     out=pre[n][:, cols], in0=sums[n, h][:], in1=b1_all[:, cols], op=ALU.add
                 )
 
         def exponential(n):
-            act[n] = wide.tile([P, HID], F32, name="act", bufs=21)
+            act[n] = wide.tile([P, HID], F32, name="act", bufs=ACTS)
             nc.scalar.activation(out=act[n][:], in_=pre[n][:], func=FUNC.Exp)
 
         def exponential_half(n, h):
             if h == 0:
-                act[n] = wide.tile([P, HID], F32, name="act", bufs=21)
+                act[n] = wide.tile([P, HID], F32, name="act", bufs=ACTS)
             cols = slice(h * BANK, (h + 1) * BANK)
             nc.scalar.activation(out=act[n][:, cols], in_=pre[n][:, cols], func=FUNC.Exp)
 
@@ -162,14 +178,14 @@ def tile_actorflowode_pb_t_kernel(tc, h0, z, k1, W1, b1, ln1_g, ln1_b, W2, b2, o
             nc.scalar.activation(out=act[n][:], in_=act[n][:], func=FUNC.Tanh)
 
         def mish(n):
+            value[n] = act[n]
             if on_gpsimd(n):
-                value[n] = wide.tile([P, HID], F32, name="value", bufs=2)
-                cols = slice(0, GPSIMD_COLS)
-                nc.gpsimd.tensor_tensor(
-                    out=value[n][:, cols], in0=pre[n][:, cols], in1=act[n][:, cols], op=ALU.mult
+                cols = slice(0, gpsimd_cols(n))
+                if gpsimd_cols(n) > 0:
+                  nc.gpsimd.tensor_tensor(
+                    out=act[n][:, cols], in0=pre[n][:, cols], in1=act[n][:, cols], op=ALU.mult
                 )
                 return
-            value[n] = act[n]
             if not squares_on_scalar(n):
                 nc.vector.tensor_tensor(out=act[n][:], in0=pre[n][:], in1=act[n][:], op=ALU.mult)
                 return
@@ -187,8 +203,15 @@ def tile_actorflowode_pb_t_kernel(tc, h0, z, k1, W1, b1, ln1_g, ln1_b, W2, b2, o
             )
 
         def mish_rest(n):
-            cols = slice(GPSIMD_COLS, HID)
-            nc.vector.tensor_tensor(
+            cols = slice(gpsimd_cols(n), HID)
+            if squares_on_scalar(n):
+                total[n] = work.tile([P, 1], F32, name="total", bufs=4)
+                nc.vector.scalar_tensor_tensor(
+                    out=act[n][:], in0=pre[n][:], scalar=1.0, in1=act[n][:],
+                    op0=ALU.mult, op1=ALU.mult, accum_out=total[n][:],
+                )
+            elif gpsimd_cols(n) < HID:
+              nc.vector.tensor_tensor(
                 out=value[n][:, cols], in0=pre[n][:, cols], in1=act[n][:, cols], op=ALU.mult
             )
 
@@ -201,11 +224,56 @@ def tile_actorflowode_pb_t_kernel(tc, h0, z, k1, W1, b1, ln1_g, ln1_b, W2, b2, o
 
         def one_over_root(n, shifted):
             rstd[n] = work.tile([P, 1], F32, name="rstd", bufs=4)
-            nc.gpsimd.tensor_tensor(out=rstd[n][:], in0=shifted[:], in1=minus_half[:], op=ALU.pow)
+            nc.gpsimd.tensor_tensor(
+                out=rstd[n][:], in0=shifted[:], in1=minus_half[:, 0:1], op=ALU.pow
+            )
 
         def aggregate(n):
-            stats[n] = work.tile([P, 2], F32, name="stats", bufs=4)
-            nc.vector.bn_aggr(out=stats[n][:], in_=partial[n][:].rearrange("p h s -> p (h s)"))
+            if not on_gpsimd(n):
+                stats[n] = work.tile([P, 2], F32, name="stats", bufs=4)
+                nc.vector.bn_aggr(out=stats[n][:], in_=partial[n][:].rearrange("p h s -> p (h s)"))
+                return
+            if n // PAIR not in pair_stats:
+                pair_stats[n // PAIR] = work.tile([P, PAIR, 2], F32, name="pair_stats", bufs=3)
+            nc.vector.bn_aggr(
+                out=pair_stats[n // PAIR][:, n % PAIR, :],
+                in_=partial[n][:].rearrange("p h s -> p (h s)"),
+            )
+
+        def shift(n):
+            k, j = n // PAIR, n % PAIR
+            if j == 0:
+                pair_shifted[k] = work.tile([P, PAIR], F32, name="pair_shifted", bufs=2)
+            if squares_on_scalar(n):
+                variance, factor = squares[n][:], 1.0 / HID
+            else:
+                variance, factor = pair_stats[k][:, j, 1:2], 1.0
+            nc.vector.tensor_scalar(
+                out=pair_shifted[k][:, j : j + 1], in0=variance, scalar1=factor, scalar2=LN_EPS,
+                op0=ALU.mult, op1=ALU.add,
+            )
+
+        def root_pair(k):
+            pair_rstd[k] = work.tile([P, PAIR], F32, name="pair_rstd", bufs=3)
+            nc.gpsimd.tensor_tensor(
+                out=pair_rstd[k][:], in0=pair_shifted[k][:], in1=minus_half[:], op=ALU.pow
+            )
+
+        def offset(n):
+            k, j = n // PAIR, n % PAIR
+            pair_offset[n] = work.tile([P, 1], F32, name="pair_offset", bufs=3)
+            mean, sign = (minus_mean[n][:], 1.0) if squares_on_scalar(n) else (pair_stats[k][:, j, 0:1], -1.0)
+            nc.vector.scalar_tensor_tensor(
+                out=pair_offset[n][:], in0=mean, scalar=sign,
+                in1=pair_rstd[k][:, j : j + 1], op0=ALU.mult, op1=ALU.mult,
+            )
+
+        def normalise_on_gpsimd(n):
+            k, j = n // PAIR, n % PAIR
+            nc.gpsimd.tensor_scalar(
+                out=act[n][:], in0=act[n][:], scalar1=pair_rstd[k][:, j : j + 1],
+                scalar2=pair_offset[n][:], op0=ALU.mult, op1=ALU.add,
+            )
 
         def finish(n, engine):
             shifted = work.tile([P, 1], F32, name="shifted", bufs=4)
@@ -228,6 +296,17 @@ def tile_actorflowode_pb_t_kernel(tc, h0, z, k1, W1, b1, ln1_g, ln1_b, W2, b2, o
                 out=shifted[:], in_=squares[n][:], func=FUNC.Identity, scale=1.0 / HID, bias=LN_EPS
             )
             one_over_root(n, shifted)
+
+        def normalise_on_vector(n):
+            k, j = n // PAIR, n % PAIR
+            if squares_on_scalar(n):
+                shift_by, op = minus_mean[n][:], ALU.add
+            else:
+                shift_by, op = pair_stats[k][:, j, 0:1], ALU.subtract
+            nc.vector.tensor_scalar(
+                out=act[n][:], in0=act[n][:], scalar1=shift_by, scalar2=pair_rstd[k][:, j : j + 1],
+                op0=op, op1=ALU.mult,
+            )
 
         def normalise(n):
             if squares_on_scalar(n):
@@ -355,10 +434,10 @@ def tile_actorflowode_pb_t_kernel(tc, h0, z, k1, W1, b1, ln1_g, ln1_b, W2, b2, o
                         in_=W1[g * K_PASS : (g + 1) * K_PASS, cols].rearrange("(p t) c -> p t c", t=PACK),
                     )
 
+            load_h0(0, LOAD)
             load_w1(0)
             nc.sync.dma_start(out=bias_row[0:1, 0:HID], in_=b1.unsqueeze(0))
             nc.sync.dma_start(out=bias_row[0:1, HID : HID + OUT], in_=b2.unsqueeze(0))
-            load_h0(0, LOAD)
             load_w1(1)
             w2_raw = keep.tile([P, PASSES, PACK, OUT], BF16, name="w2_raw")
             nc.scalar.dma_start(
@@ -367,7 +446,7 @@ def tile_actorflowode_pb_t_kernel(tc, h0, z, k1, W1, b1, ln1_g, ln1_b, W2, b2, o
             for first in range(LOAD, LOADS * LOAD, LOAD):
                 load_h0(first, LOAD)
 
-            for h in range(HALVES):
+            def spread_b1(h):
                 cols = slice(h * BANK, (h + 1) * BANK)
                 spread = psum.tile([P, BANK], F32, name="acc", bufs=ACC)
                 nc.tensor.matmul(out=spread[:], lhsT=ones[:], rhs=bias_row[:, cols], start=True, stop=True)
@@ -378,13 +457,14 @@ def tile_actorflowode_pb_t_kernel(tc, h0, z, k1, W1, b1, ln1_g, ln1_b, W2, b2, o
 
             w1_grouped = {}
 
-            def regroup_w1(g, h, copy):
-                w1_grouped[g, h] = prep.tile(
-                    [P, BANK, PACK], BF16, name="w1_grouped", bufs=PASSES * HALVES, align_bytes=64
-                )
+            def regroup_w1(g, h, copy, m0=0, m1=P):
+                if (g, h) not in w1_grouped:
+                    w1_grouped[g, h] = prep.tile(
+                        [P, BANK, PACK], BF16, name="w1_grouped", bufs=PASSES * HALVES, align_bytes=64
+                    )
                 copy(
-                    out=w1_grouped[g, h][:].rearrange("p (t m) j -> p t m j", t=PACK),
-                    in_=w1_raw[g, h][:].rearrange("p j (m t) -> p t m j", t=PACK),
+                    out=w1_grouped[g, h][:].rearrange("p (t m) j -> p t m j", t=PACK)[:, :, m0:m1, :],
+                    in_=w1_raw[g, h][:].rearrange("p j (m t) -> p t m j", t=PACK)[:, :, m0:m1, :],
                 )
 
             def pack_w1(g, h):
@@ -395,28 +475,32 @@ def tile_actorflowode_pb_t_kernel(tc, h0, z, k1, W1, b1, ln1_g, ln1_b, W2, b2, o
                     in_=w1_grouped[g, h][:].rearrange("p c t -> p (c t)"),
                 )
 
-            for g in range(PASSES):
-                regroup_w1(g, 0, nc.vector.tensor_copy)
-            for n in range(2):
-                turn_h0(n)
-                group_h0(n, nc.scalar.copy)
-            for g in range(PASSES):
-                pack_w1(g, 0)
-            for n in range(2):
-                pack_h0(n)
-                first_layer(n, [0])
-            regroup_w1(0, 1, nc.scalar.copy)
+            turn_h0(0)
+            group_h0(0, nc.vector.tensor_copy)
+            turn_h0(1)
+            group_h0(1, nc.scalar.copy)
+            pack_h0(0)
+            regroup_w1(1, 0, nc.scalar.copy, 0, 96)
+            regroup_w1(0, 0, nc.vector.tensor_copy)
+            pack_h0(1)
+            pack_w1(0, 0)
+            regroup_w1(1, 0, nc.vector.tensor_copy, 96, P)
+            pack_w1(1, 0)
+            spread_b1(0)
+            spread_b1(1)
+            first_layer(0, [0])
+            first_layer(1, [0])
+            regroup_w1(1, 1, nc.scalar.copy, 0, 96)
+            regroup_w1(0, 1, nc.vector.tensor_copy)
+            pack_w1(0, 1)
             add_bias(0, [0])
-            regroup_w1(1, 1, nc.vector.tensor_copy)
+            regroup_w1(1, 1, nc.vector.tensor_copy, 96, P)
             add_bias(1, [0])
-            for n in range(2, 6):
-                turn_h0(n)
-                group_h0(n, nc.scalar.copy)
-            turn_h0(6)
-            turn_h0(7)
-            for g in range(PASSES):
-                pack_w1(g, 1)
-
+            pack_w1(1, 1)
+            turn_h0(2)
+            group_h0(2, nc.scalar.copy)
+            turn_h0(3)
+            group_h0(3, nc.scalar.copy)
         def prepare_w2():
             w2_grouped = work.tile([P, PASSES, OUT, PACK], BF16, name="w2_grouped", align_bytes=64)
             for g in range(PASSES):
@@ -470,51 +554,70 @@ def tile_actorflowode_pb_t_kernel(tc, h0, z, k1, W1, b1, ln1_g, ln1_b, W2, b2, o
             if live(n):
                 first_layer(n)
 
-        for n in range(GROUP):
-            if n < 2:
-                if n == 0:
-                    exponential_half(0, 0)
-                    exponential_half(1, 0)
-                    first_layer(0, [1])
-                add_bias(n, [1])
-                exponential_half(n, 1)
-            else:
-                add_bias(n)
-                exponential(n)
-            if n + 1 < GROUP:
-                first_layer(n + 1, range(HALVES) if n > 0 else [1])
-            if n + 2 < GROUP:
+        first_group = [8, 8, 8, 8][0]
+        exponential_half(0, 0)
+        exponential_half(1, 0)
+        for n in range(4, 8):
+            turn_h0(n)
+            group_h0(n, nc.scalar.copy) if n < 8 else None
+        for n in range(2):
+            first_layer(n, [1])
+        pack_h0(2)
+        add_bias(0, [1])
+        exponential_half(0, 1)
+        pack_h0(3)
+        first_layer(2)
+        add_bias(1, [1])
+        exponential_half(1, 1)
+        for n in range(2, first_group):
+            if n + 2 < 8:
                 pack_h0(n + 2)
-            if n + 6 < GROUP:
-                group_h0(n + 6, nc.scalar.copy)
-        for n in range(GROUP):
+            if n + 1 < 8:
+                first_layer(n + 1)
+            add_bias(n)
+            exponential(n)
+        for n in range(first_group):
             softplus(n)
         prepare_w2()
-        added = GROUP + LEAD
-        for k in range(GROUP, added + 4):
-            turn(k)
-            if k - 4 >= GROUP:
-                add_bias(k - 4)
-            if GROUP <= k - 1 < added + 3:
-                group(k - 1, nc.vector.tensor_copy)
-            if k - 3 >= GROUP:
-                multiply(k - 3)
-            if GROUP <= k - 2 < added + 2:
-                pack(k - 2)
+        added = first_group + LEAD
+        for n in range(4, added):
+            if n + 4 >= 8:
+                turn(n + 4)
+            if n + 3 >= 8:
+                group(n + 3, nc.vector.tensor_copy)
+            if n + 1 >= min(first_group + 1, 8):
+                multiply(n + 1)
+            if n >= first_group:
+                add_bias(n)
+            if n + 2 >= min(first_group + 2, 8):
+                pack(n + 2)
 
-        activations = []
-        for first in range(0, TILES, GROUP):
-            for n in range(first, first + GROUP):
-                activations.append((tanh, n))
-                if live(n + GROUP):
-                    activations.append((exponential, n + GROUP))
-            for n in range(first + GROUP, first + 2 * GROUP):
-                if live(n):
-                    activations.append((softplus, n))
+        groups = [8, 8, 8, 8]
+        per_step = [[] for n in range(TILES)]
+        first = 0
+        for g, size in enumerate(groups):
+            acts = []
+            follow = groups[g + 1] if g + 1 < len(groups) else 0
+            x = [(tanh, first + j) for j in range(size)]
+            y = [(exponential, first + size + j) for j in range(follow)]
+            for j in range(max(size, follow)):
+                acts += x[j : j + 1] + y[j : j + 1]
+            acts += [(softplus, first + size + j) for j in range(follow)]
+            if g == len(groups) - 2:
+                acts.append((tanh, first + size))
+            if g == len(groups) - 1:
+                acts = acts[1:]
+                for j in range(size - 1):
+                    per_step[first + j] = acts[j : j + 1]
+                continue
+            for j in range(size):
+                per_step[first + j] = acts[j * len(acts) // size : (j + 1) * len(acts) // size]
+            first += size
 
         units = [range(n, n + QUAD) for n in range(0, TILES - QUAD, QUAD)]
         units += [range(TILES - QUAD, TILES - 2), range(TILES - 2, TILES)]
-        starts = [unit[-1] + (4 if squares_on_scalar(unit[-1]) else 3) for unit in units]
+        starts = [unit[-1] + 4 for unit in units[:-2]]
+        starts += [starts[-1] + QUAD, starts[-1] + QUAD + 2]
 
         def banks_of(i):
             return [
@@ -524,85 +627,109 @@ def tile_actorflowode_pb_t_kernel(tc, h0, z, k1, W1, b1, ln1_g, ln1_b, W2, b2, o
                 if 0 <= i - start < len(unit)
             ]
 
+        def vector_takes(i, k):
+            if live(i + added):
+                return k == 1 and i % 2 == 0
+            if live(i + groups[-1]):
+                return k == 1 and i % 2 == 1
+            return False
+
+        def work_on_head(i, lag, stage):
+            for unit, start in zip(units, starts):
+                if i == start + lag(len(unit)):
+                    stage(unit)
+
         for i in range(starts[-1] + len(units[-1]) + 3):
             a = i + added
-            share = 3 if live(i + GROUP) else 1
-            now, activations = activations[:share], activations[share:]
+            early = live(a)
+            now = per_step[i] if live(i) else []
             banks = banks_of(i)
-            vector_helps = not live(a) and live(i + GROUP)
-            for unit, start in zip(units, starts):
-                if i == start - 2:
-                    load_base(unit)
-                if i == start + 1:
-                    copy_base(unit)
+            vector_banks = [k for k in range(len(banks)) if vector_takes(i, k)]
+            work_on_head(i, lambda w: -2, load_base)
             for k in range(max(len(now), len(banks))):
                 if k < len(now):
                     stage, n = now[k]
                     stage(n)
                 if k == min(1, len(now)) and live(i - 1) and squares_on_scalar(i - 1):
                     sum_squares(i - 1)
-                if k < len(banks) and not (vector_helps and k % 2 == 1):
+                if k < len(banks) and k not in vector_banks:
                     scale_act(*banks[k], False)
-            if live(i - 1) and squares_on_scalar(i - 1):
-                finish_on_scalar(i - 1)
-            if live(i - 2) and on_gpsimd(i - 2):
-                normalise(i - 2)
-            early = live(a)
-            if early:
+            work_on_head(i, lambda w: 1, copy_base)
+            def early_step():
+                if live(i - 3):
+                    offset(i - 3)
+                    normalise_on_gpsimd(i - 3)
+                mish(i)
+                if live(i - 1):
+                    partial_statistics(i - 1)
                 for unit, bank in banks_of(i + 1):
                     turn_act(unit, bank)
-                for unit, start in zip(units, starts):
-                    if i == start:
-                        add_base(unit)
-            if live(i) and on_gpsimd(i):
-                mish(i)
-            if live(i - 1) and on_gpsimd(i - 1):
-                partial_statistics(i - 1)
-                aggregate(i - 1)
-                finish(i - 1, nc.gpsimd)
-            if live(a):
-                add_bias(a)
-            group(a + 3, nc.vector.tensor_copy)
-            if early:
-                for unit, start in zip(units, starts):
-                    if i == start + len(unit) + 2:
-                        corrector(unit)
-            multiply(a + 1)
-            turn(a + 4)
-            if live(i) and not on_gpsimd(i):
-                mish(i)
-            if live(i - 1) and not squares_on_scalar(i - 1) and not on_gpsimd(i - 1):
-                finish(i - 1, nc.vector)
-            if vector_helps:
-                for unit, bank in banks[1::2]:
-                    scale_act(unit, bank, True)
-            pack(a + 2)
-            for unit, start in zip(units, starts):
-                if i == start and not early:
-                    add_base(unit)
-                if i == start + len(unit) // 2 + 1:
-                    pack_h1(unit, 0)
-                if i == start + len(unit) + 1:
-                    pack_h1(unit, 1)
-                    second_layer(unit)
-                if i == start + len(unit) // 2:
-                    group_h1(unit, 0)
-                if i == start + len(unit):
-                    group_h1(unit, 1)
-                if i == start + len(unit) + 2 and not early:
-                    corrector(unit)
-            if live(i) and squares_on_scalar(i):
-                find_mean(i)
-            if live(i) and on_gpsimd(i):
+                work_on_head(i, lambda w: 0, add_base)
+                add_bias(a, [0])
+                if live(i - 1):
+                    aggregate(i - 1)
+                add_bias(a, [1])
+                if live(i - 1):
+                    shift(i - 1)
+                    if (i - 1) % PAIR == PAIR - 1:
+                        root_pair((i - 1) // PAIR)
+                for k in vector_banks:
+                    scale_act(*banks[k], True)
+                multiply(a + 1)
+                group(a + 3, nc.vector.tensor_copy)
+                work_on_head(i, lambda w: w + 2, corrector)
+                turn(a + 4)
+                pack(a + 2)
+                head_work()
                 mish_rest(i)
-            if live(i) and not squares_on_scalar(i) and not on_gpsimd(i):
-                partial_statistics(i)
-            if live(i - 2) and squares_on_scalar(i - 2):
-                normalise(i - 2)
-            if live(i - 1) and not squares_on_scalar(i - 1) and not on_gpsimd(i - 1):
-                normalise(i - 1)
-            if live(i) and not squares_on_scalar(i) and not on_gpsimd(i):
-                aggregate(i)
-            if not early:
+
+            def head_work():
+                work_on_head(i, lambda w: w // 2 + 1, lambda u: pack_h1(u, 0))
+                work_on_head(i, lambda w: w + 1, lambda u: pack_h1(u, 1))
+                work_on_head(i, lambda w: w + 1, second_layer)
+                work_on_head(i, lambda w: w // 2, lambda u: group_h1(u, 0))
+                work_on_head(i, lambda w: w, lambda u: group_h1(u, 1))
+
+            def late_step():
+                n = i - 3
+                on_g = live(n) and gpsimd_normalises(n)
+                counted = live(i - 1) and not squares_on_scalar(i - 1)
+                root_now = n % PAIR == 0 and n >= TILES - added - PAIR and live(n)
+                if root_now:
+                    root_pair(n // PAIR)
+                elif on_g:
+                    offset(n)
+                    normalise_on_gpsimd(n)
+                if live(i):
+                    mish(i)
+                if counted:
+                    partial_statistics(i - 1)
+                if counted and not root_now:
+                    aggregate(i - 1)
+                for k in vector_banks:
+                    scale_act(*banks[k], True)
+                if counted and root_now:
+                    aggregate(i - 1)
+                if root_now and on_g:
+                    offset(n)
+                    normalise_on_gpsimd(n)
+                if live(i):
+                    mish_rest(i)
+                if counted:
+                    shift(i - 1)
+                if live(n) and not on_g:
+                    normalise_on_vector(n)
+                if live(i) and squares_on_scalar(i):
+                    find_mean(i)
                 for unit, bank in banks_of(i + 1):
                     turn_act(unit, bank)
+                work_on_head(i, lambda w: 0, add_base)
+                work_on_head(i, lambda w: w + 2, corrector)
+                head_work()
+                if live(i - 1) and squares_on_scalar(i - 1):
+                    shift(i - 1)
+
+            if early:
+                early_step()
+            else:
+                late_step()

@@ -69,16 +69,18 @@ def tile_actorflowode_pb_t_kernel(tc, h0, z, k1, W1, b1, ln1_g, ln1_b, W2, b2, o
         def gpsimd_cols(n):
             if squares_on_scalar(n):
                 return 0
-            return GPSIMD_COLS if live(n + added) else GPSIMD_COLS_LATE
+            if live(n + added):
+                return 704 if n % 2 == 1 else 576
+            return GPSIMD_COLS_LATE
 
         def live(n):
             return 0 <= n < TILES
 
         def gpsimd_normalises(n):
-            return n < 21
+            return n < 24
 
         def squares_on_scalar(n):
-            return n >= 24 and n % 2 == 1
+            return n >= 24
 
         state, act_turned, base_bank = {}, {}, {}
         h0_sb, h0_turned, h0_grouped, h0_codes, h0_scales = {}, {}, {}, {}, {}
@@ -480,11 +482,11 @@ def tile_actorflowode_pb_t_kernel(tc, h0, z, k1, W1, b1, ln1_g, ln1_b, W2, b2, o
             turn_h0(1)
             group_h0(1, nc.scalar.copy)
             pack_h0(0)
-            regroup_w1(1, 0, nc.scalar.copy, 0, 96)
+            regroup_w1(1, 0, nc.scalar.copy, 0, 64)
             regroup_w1(0, 0, nc.vector.tensor_copy)
             pack_h0(1)
             pack_w1(0, 0)
-            regroup_w1(1, 0, nc.vector.tensor_copy, 96, P)
+            regroup_w1(1, 0, nc.vector.tensor_copy, 64, P)
             pack_w1(1, 0)
             spread_b1(0)
             spread_b1(1)
@@ -631,8 +633,8 @@ def tile_actorflowode_pb_t_kernel(tc, h0, z, k1, W1, b1, ln1_g, ln1_b, W2, b2, o
             if live(i + added):
                 return k == 1 and i % 2 == 0
             if live(i + groups[-1]):
-                return k == 1 and i % 2 == 1
-            return False
+                return k == 1 and (i % 2 == 1 or i == 22)
+            return k == 1 and i % 2 == 1 and i < 32
 
         def work_on_head(i, lag, stage):
             for unit, start in zip(units, starts):

@@ -70,14 +70,14 @@ def tile_actorflowode_pb_t_kernel(tc, h0, z, k1, W1, b1, ln1_g, ln1_b, W2, b2, o
             if squares_on_scalar(n):
                 return 0
             if live(n + added):
-                return 704 if n % 2 == 1 else 576
+                return 576 if n % 2 == 1 else 448
             return GPSIMD_COLS_LATE
 
         def live(n):
             return 0 <= n < TILES
 
         def gpsimd_normalises(n):
-            return n < 24
+            return n < 20
 
         def squares_on_scalar(n):
             return n >= 24
@@ -98,6 +98,12 @@ def tile_actorflowode_pb_t_kernel(tc, h0, z, k1, W1, b1, ln1_g, ln1_b, W2, b2, o
         make_identity(nc, ident[:])
         ident_bf16 = keep.tile([P, P], BF16, name="ident_bf16")
         make_identity(nc, ident_bf16[:])
+        partials = []
+        for r in range(3):
+            ring = keep.tile([P, 6 * HALVES + 3], F32, name="partial_" + str(r))
+            nc.vector.memset(ring[:], 0.0)
+            nc.vector.memset(ring[:, 6 * HALVES + 2 :], LN_EPS * HID)
+            partials.append(ring)
         ones = keep.tile([P, P], BF16, name="ones")
         nc.vector.memset(ones[:], 1.0)
         minus_half = keep.tile([P, PAIR], F32, name="minus_half")
@@ -218,10 +224,10 @@ def tile_actorflowode_pb_t_kernel(tc, h0, z, k1, W1, b1, ln1_g, ln1_b, W2, b2, o
             )
 
         def partial_statistics(n):
-            partial[n] = work.tile([P, HALVES, 6], F32, name="partial", bufs=4)
+            partial[n] = partials[n % len(partials)]
             for h in range(HALVES):
                 nc.vector.bn_stats(
-                    out=partial[n][:, h, :], in_=value[n][:, h * BANK : (h + 1) * BANK]
+                    out=partial[n][:, 6 * h : 6 * (h + 1)], in_=value[n][:, h * BANK : (h + 1) * BANK]
                 )
 
         def one_over_root(n, shifted):
@@ -239,11 +245,13 @@ def tile_actorflowode_pb_t_kernel(tc, h0, z, k1, W1, b1, ln1_g, ln1_b, W2, b2, o
                 pair_stats[n // PAIR] = work.tile([P, PAIR, 2], F32, name="pair_stats", bufs=3)
             nc.vector.bn_aggr(
                 out=pair_stats[n // PAIR][:, n % PAIR, :],
-                in_=partial[n][:].rearrange("p h s -> p (h s)"),
+                in_=partial[n][:],
             )
 
         def shift(n):
             k, j = n // PAIR, n % PAIR
+            if not squares_on_scalar(n):
+                return
             if j == 0:
                 pair_shifted[k] = work.tile([P, PAIR], F32, name="pair_shifted", bufs=2)
             if squares_on_scalar(n):
@@ -257,8 +265,9 @@ def tile_actorflowode_pb_t_kernel(tc, h0, z, k1, W1, b1, ln1_g, ln1_b, W2, b2, o
 
         def root_pair(k):
             pair_rstd[k] = work.tile([P, PAIR], F32, name="pair_rstd", bufs=3)
+            shifted = pair_shifted[k][:] if squares_on_scalar(PAIR * k) else pair_stats[k][:, :, 1]
             nc.gpsimd.tensor_tensor(
-                out=pair_rstd[k][:], in0=pair_shifted[k][:], in1=minus_half[:], op=ALU.pow
+                out=pair_rstd[k][:], in0=shifted, in1=minus_half[:], op=ALU.pow
             )
 
         def offset(n):

@@ -362,7 +362,9 @@ def tile_actorflowode_pb_t_kernel(tc, h0, z, k1, W1, b1, ln1_g, ln1_b, W2, b2, o
             h1_grouped[unit, g] = work.tile(
                 [P, len(unit) * P, PACK], BF16, name="h1_grouped", bufs=PASSES, align_bytes=64
             )
-            interleave_four(nc.vector.tensor_copy, h1_grouped[unit, g][:], h1[unit, g][:])
+            on_scalar = unit[-1] == TILES - 1 and g == 1
+            copy = nc.scalar.copy if on_scalar else nc.vector.tensor_copy
+            interleave_four(copy, h1_grouped[unit, g][:], h1[unit, g][:])
 
         def pack_h1(unit, g):
             width = len(unit) * P
@@ -568,11 +570,14 @@ def tile_actorflowode_pb_t_kernel(tc, h0, z, k1, W1, b1, ln1_g, ln1_b, W2, b2, o
         first_group = [8, 8, 8, 8][0]
         exponential_half(0, 0)
         exponential_half(1, 0)
-        for n in range(4, 8):
+        for n in range(4, 6):
             turn_h0(n)
-            group_h0(n, nc.scalar.copy) if n < 8 else None
+            group_h0(n, nc.scalar.copy)
         for n in range(2):
             first_layer(n, [1])
+        for n in range(6, 8):
+            turn_h0(n)
+            group_h0(n, nc.scalar.copy)
         pack_h0(2)
         add_bias(0, [1])
         exponential_half(0, 1)

@@ -40,8 +40,8 @@ FLOPS = 2 * BATCH * HID * (HID + OUT)
 
 def interleave_four(copy, dst, src):
     copy(
-        out=dst.rearrange("p (c i) t -> p c t i", i=4),
-        in_=src.rearrange("p t (c i) -> p c t i", i=4),
+        out=dst.rearrange("p (c i) t -> p c t i", i=8),
+        in_=src.rearrange("p t (c i) -> p c t i", i=8),
     )
 
 

from contextlib import ExitStack

import concourse.mybir as mybir
from concourse.masks import make_identity

F32 = mybir.dt.float32
BF16 = mybir.dt.bfloat16
U32 = mybir.dt.uint32
U8 = mybir.dt.uint8
FP8X4 = mybir.dt.float8_e4m3fn_x4
FUNC = mybir.ActivationFunctionType
ALU = mybir.AluOpType

P = 128
BATCH, HID, OUT = 4096, 1024, 128
TILES = BATCH // P
QUAD = 4
QUADS = TILES // QUAD
PACK = 4
K_PASS = P * PACK
PASSES = HID // K_PASS
BANK = 512
HALVES = HID // BANK
LOAD = 2
ACC = 3
TURNED = 4
GPSIMD_COLS = 704
GPSIMD_COLS_LATE = 0
ACTS = 22
PRES = 14
PAIR = 2
LOADS = 3
GROUP = 8
U_TILES = HID // P
LN_EPS = 1e-5
STEP = 0.25

FLOPS = 2 * BATCH * HID * (HID + OUT)


def interleave_four(copy, dst, src):
    copy(
        out=dst.rearrange("p (c i) t -> p c t i", i=8),
        in_=src.rearrange("p t (c i) -> p c t i", i=8),
    )


def tile_actorflowode_pb_t_kernel(tc, h0, z, k1, W1, b1, ln1_g, ln1_b, W2, b2, out):
    nc = tc.nc
    h0_rows = h0.rearrange("(p n) k -> p n k", n=TILES)
    z_rows = z.rearrange("(p n) c -> p n c", n=TILES)
    k1_rows = k1.rearrange("(p n) c -> p n c", n=TILES)
    out_rows = out.rearrange("(p n) c -> p n c", n=TILES)

    with ExitStack() as ctx:
        ctx.enter_context(tc.manual_schedule())
        keep = ctx.enter_context(tc.tile_pool(name="keep", bufs=1))
        feed = ctx.enter_context(tc.tile_pool(name="feed", bufs=1))
        wide = ctx.enter_context(tc.tile_pool(name="wide", bufs=1))
        psum = ctx.enter_context(tc.psum_pool(name="psum", bufs=1))

        LEAD = 5
        total, minus_mean, squares = {}, {}, {}
        value = {}

        def on_gpsimd(n):
            return n < 32

        def gpsimd_cols(n):
            if squares_on_scalar(n):
                return 0
            if live(n + added):
                return 576 if n % 2 == 1 else 448
            return GPSIMD_COLS_LATE

        def live(n):
            return 0 <= n < TILES

        def gpsimd_normalises(n):
            return n < 20

        def squares_on_scalar(n):
            return n >= 24

        state, act_turned, base_bank = {}, {}, {}
        h0_sb, h0_turned, h0_grouped, h0_codes, h0_scales = {}, {}, {}, {}, {}
        sums, pre, act, partial, stats, rstd = {}, {}, {}, {}, {}, {}
        pair_stats, pair_shifted, pair_rstd, pair_offset = {}, {}, {}, {}
        h1, h1_grouped, h1_codes, h1_scales, head, base = {}, {}, {}, {}, {}, {}

        def load_h0(first, count):
            rows = feed.tile([P, LOAD, HID], BF16, name="h0_sb", bufs=LOADS)
            nc.sync.dma_start(out=rows[:, 0:count, :], in_=h0_rows[:, first : first + count, :])
            for j in range(count):
                h0_sb[first + j] = rows[:, j, :]

        ident = keep.tile([P, P], F32, name="ident")
        make_identity(nc, ident[:])
        ident_bf16 = keep.tile([P, P], BF16, name="ident_bf16")
        make_identity(nc, ident_bf16[:])
        partials = []
        for r in range(3):
            ring = keep.tile([P, 6 * HALVES + 3], F32, name="partial_" + str(r))
            nc.vector.memset(ring[:], 0.0)
            nc.vector.memset(ring[:, 6 * HALVES + 2 :], LN_EPS * HID)
            partials.append(ring)
        ones = keep.tile([P, P], BF16, name="ones")
        nc.vector.memset(ones[:], 1.0)
        minus_half = keep.tile([P, PAIR], F32, name="minus_half")
        nc.vector.memset(minus_half[:], -0.5)
        bias_row = keep.tile([P, HID + OUT], BF16, name="bias_row")
        nc.vector.memset(bias_row[:], 0.0)
        gain_rows = keep.tile([P, PASSES, PACK], BF16, name="gain_rows")
        shift_rows = keep.tile([P, PASSES, PACK], BF16, name="shift_rows")

        for rows, vector in ((gain_rows, ln1_g), (shift_rows, ln1_b)):
            nc.scalar.dma_start(out=rows[:], in_=vector.rearrange("(g p t) -> p g t", p=P, t=PACK))

        def turn_h0(n):
            words = h0_sb[n].bitcast(F32)
            h0_turned[n] = psum.tile([P, PACK, P], F32, name="turned", bufs=TURNED)
            for g in range(PASSES):
                for u in range(2):
                    nc.tensor.transpose(
                        h0_turned[n][:, 2 * g + u, :],
                        words[:, 2 * P * g + u : 2 * P * (g + 1) : 2],
                        ident[:],
                    )
            if (n + 1) % LOAD == 0 and n + 1 + (LOADS - 1) * LOAD < TILES:
                load_h0(n + 1 + (LOADS - 1) * LOAD, LOAD)

        def group_h0(n, copy):
            h0_grouped[n] = feed.tile([P, HID], BF16, name="h0_grouped", bufs=4, align_bytes=64)
            copy(
                out=h0_grouped[n][:].bitcast(F32).rearrange("p (g r u) -> p g r u", g=PASSES, u=2),
                in_=h0_turned[n][:].rearrange("p (g u) r -> p g r u", u=2),
            )

        def pack_h0(n):
            h0_codes[n] = feed.tile([P, PASSES * P], U32, name="h0_codes", bufs=4, align_bytes=64)
            h0_scales[n] = feed.tile([P, PASSES * P], U8, name="h0_scales", bufs=4, align_bytes=64)
            nc.vector.quantize_mx(
                out=h0_codes[n][:].bitcast(FP8X4), scales=h0_scales[n][:], in_=h0_grouped[n][:]
            )

        def first_layer(n, halves=range(HALVES)):
            for h in halves:
                cols = slice(h * BANK, (h + 1) * BANK)
                acc = psum.tile([P, BANK], F32, name="acc", bufs=ACC)
                sums[n, h] = acc
                for g in range(PASSES):
                    rows = slice(g * P, (g + 1) * P)
                    nc.tensor.matmul_mx(
                        out=acc[:],
                        lhsT=h0_codes[n][:, rows].bitcast(FP8X4),
                        lhsT_scale=h0_scales[n][:, rows],
                        rhs=w1_codes[g, h][:].bitcast(FP8X4),
                        rhs_scale=w1_scales[g, h][:],
                        start=(g == 0),
                        stop=(g == PASSES - 1),
                    )

        def add_bias(n, halves=range(HALVES)):
            for h in halves:
                if h == 0:
                    pre[n] = wide.tile([P, HID], F32, name="pre", bufs=PRES)
                cols = slice(h * BANK, (h + 1) * BANK)
                nc.vector.tensor_tensor(
                    out=pre[n][:, cols], in0=sums[n, h][:], in1=b1_all[:, cols], op=ALU.add
                )

        def exponential(n):
            act[n] = wide.tile([P, HID], F32, name="act", bufs=ACTS)
            nc.scalar.activation(out=act[n][:], in_=pre[n][:], func=FUNC.Exp)

        def exponential_half(n, h):
            if h == 0:
                act[n] = wide.tile([P, HID], F32, name="act", bufs=ACTS)
            cols = slice(h * BANK, (h + 1) * BANK)
            nc.scalar.activation(out=act[n][:, cols], in_=pre[n][:, cols], func=FUNC.Exp)

        def softplus(n):
            nc.scalar.activation(out=act[n][:], in_=act[n][:], func=FUNC.Ln, bias=1.0)

        def tanh(n):
            nc.scalar.activation(out=act[n][:], in_=act[n][:], func=FUNC.Tanh)

        def mish(n):
            value[n] = act[n]
            if on_gpsimd(n):
                cols = slice(0, gpsimd_cols(n))
                if gpsimd_cols(n) > 0:
                  nc.gpsimd.tensor_tensor(
                    out=act[n][:, cols], in0=pre[n][:, cols], in1=act[n][:, cols], op=ALU.mult
                )
                return
            if not squares_on_scalar(n):
                nc.vector.tensor_tensor(out=act[n][:], in0=pre[n][:], in1=act[n][:], op=ALU.mult)
                return
            total[n] = work.tile([P, 1], F32, name="total", bufs=4)
            nc.vector.scalar_tensor_tensor(
                out=act[n][:], in0=pre[n][:], scalar=1.0, in1=act[n][:],
                op0=ALU.mult, op1=ALU.mult, accum_out=total[n][:],
            )

        def find_mean(n):
            minus_mean[n] = work.tile([P, 1], F32, name="minus_mean", bufs=4)
            nc.vector.tensor_scalar(
                out=minus_mean[n][:], in0=total[n][:], scalar1=-1.0 / HID, scalar2=0.0,
                op0=ALU.mult, op1=ALU.add,
            )

        def mish_rest(n):
            cols = slice(gpsimd_cols(n), HID)
            if squares_on_scalar(n):
                total[n] = work.tile([P, 1], F32, name="total", bufs=4)
                nc.vector.scalar_tensor_tensor(
                    out=act[n][:], in0=pre[n][:], scalar=1.0, in1=act[n][:],
                    op0=ALU.mult, op1=ALU.mult, accum_out=total[n][:],
                )
            elif gpsimd_cols(n) < HID:
              nc.vector.tensor_tensor(
                out=value[n][:, cols], in0=pre[n][:, cols], in1=act[n][:, cols], op=ALU.mult
            )

        def partial_statistics(n):
            partial[n] = partials[n % len(partials)]
            for h in range(HALVES):
                nc.vector.bn_stats(
                    out=partial[n][:, 6 * h : 6 * (h + 1)], in_=value[n][:, h * BANK : (h + 1) * BANK]
                )

        def one_over_root(n, shifted):
            rstd[n] = work.tile([P, 1], F32, name="rstd", bufs=4)
            nc.gpsimd.tensor_tensor(
                out=rstd[n][:], in0=shifted[:], in1=minus_half[:, 0:1], op=ALU.pow
            )

        def aggregate(n):
            if not on_gpsimd(n):
                stats[n] = work.tile([P, 2], F32, name="stats", bufs=4)
                nc.vector.bn_aggr(out=stats[n][:], in_=partial[n][:].rearrange("p h s -> p (h s)"))
                return
            if n // PAIR not in pair_stats:
                pair_stats[n // PAIR] = work.tile([P, PAIR, 2], F32, name="pair_stats", bufs=3)
            nc.vector.bn_aggr(
                out=pair_stats[n // PAIR][:, n % PAIR, :],
                in_=partial[n][:],
            )

        def shift(n):
            k, j = n // PAIR, n % PAIR
            if not squares_on_scalar(n):
                return
            if j == 0:
                pair_shifted[k] = work.tile([P, PAIR], F32, name="pair_shifted", bufs=2)
            if squares_on_scalar(n):
                variance, factor = squares[n][:], 1.0 / HID
            else:
                variance, factor = pair_stats[k][:, j, 1:2], 1.0
            nc.vector.tensor_scalar(
                out=pair_shifted[k][:, j : j + 1], in0=variance, scalar1=factor, scalar2=LN_EPS,
                op0=ALU.mult, op1=ALU.add,
            )

        def root_pair(k):
            pair_rstd[k] = work.tile([P, PAIR], F32, name="pair_rstd", bufs=3)
            shifted = pair_shifted[k][:] if squares_on_scalar(PAIR * k) else pair_stats[k][:, :, 1]
            nc.gpsimd.tensor_tensor(
                out=pair_rstd[k][:], in0=shifted, in1=minus_half[:], op=ALU.pow
            )

        def offset(n):
            k, j = n // PAIR, n % PAIR
            pair_offset[n] = work.tile([P, 1], F32, name="pair_offset", bufs=3)
            mean, sign = (minus_mean[n][:], 1.0) if squares_on_scalar(n) else (pair_stats[k][:, j, 0:1], -1.0)
            nc.vector.scalar_tensor_tensor(
                out=pair_offset[n][:], in0=mean, scalar=sign,
                in1=pair_rstd[k][:, j : j + 1], op0=ALU.mult, op1=ALU.mult,
            )

        def normalise_on_gpsimd(n):
            k, j = n // PAIR, n % PAIR
            nc.gpsimd.tensor_scalar(
                out=act[n][:], in0=act[n][:], scalar1=pair_rstd[k][:, j : j + 1],
                scalar2=pair_offset[n][:], op0=ALU.mult, op1=ALU.add,
            )

        def finish(n, engine):
            shifted = work.tile([P, 1], F32, name="shifted", bufs=4)
            engine.tensor_scalar(
                out=shifted[:], in0=stats[n][:, 1:2], scalar1=1.0, scalar2=LN_EPS,
                op0=ALU.mult, op1=ALU.add,
            )
            one_over_root(n, shifted)

        def sum_squares(n):
            squares[n] = work.tile([P, 1], F32, name="squares", bufs=4)
            nc.scalar.activation(
                out=pre[n][:], in_=act[n][:], func=FUNC.Square, bias=minus_mean[n][:],
                accum_out=squares[n][:],
            )

        def finish_on_scalar(n):
            shifted = work.tile([P, 1], F32, name="shifted_squares", bufs=4)
            nc.scalar.activation(
                out=shifted[:], in_=squares[n][:], func=FUNC.Identity, scale=1.0 / HID, bias=LN_EPS
            )
            one_over_root(n, shifted)

        def normalise_on_vector(n):
            k, j = n // PAIR, n % PAIR
            if squares_on_scalar(n):
                shift_by, op = minus_mean[n][:], ALU.add
            else:
                shift_by, op = pair_stats[k][:, j, 0:1], ALU.subtract
            nc.vector.tensor_scalar(
                out=act[n][:], in0=act[n][:], scalar1=shift_by, scalar2=pair_rstd[k][:, j : j + 1],
                op0=op, op1=ALU.mult,
            )

        def normalise(n):
            if squares_on_scalar(n):
                shift, op = minus_mean[n][:], ALU.add
            else:
                shift, op = stats[n][:, 0:1], ALU.subtract
            nc.vector.tensor_scalar(
                out=act[n][:], in0=value[n][:], scalar1=shift, scalar2=rstd[n][:],
                op0=op, op1=ALU.mult,
            )

        def turn_act(unit, bank):
            blocks = BANK // (len(unit) * P)
            turned = psum.tile([P, blocks, len(unit), P], F32, name="turned", bufs=TURNED)
            act_turned[unit, bank] = turned
            for b in range(blocks):
                u = bank * blocks + b
                for j, n in enumerate(unit):
                    nc.tensor.transpose(turned[:, b, j, :], act[n][:, u * P : (u + 1) * P], ident[:])

        def scale_act(unit, bank, on_vector):
            width = len(unit) * P
            blocks = BANK // width
            if bank * blocks % PACK == 0:
                h1[unit, bank * blocks // PACK] = work.tile([P, PACK, width], BF16, name="h1", bufs=3)
            for b in range(blocks):
                u = bank * blocks + b
                turned = act_turned[unit, bank][:, b, :, :].rearrange("p j r -> p (j r)")
                gain, shift = gains[:, u : u + 1], gains[:, U_TILES + u : U_TILES + u + 1]
                if on_vector:
                    nc.vector.tensor_scalar(
                        out=h1[unit, u // PACK][:, u % PACK, :], in0=turned,
                        scalar1=gain, scalar2=shift, op0=ALU.mult, op1=ALU.add,
                    )
                else:
                    nc.scalar.activation(
                        out=h1[unit, u // PACK][:, u % PACK, :], in_=turned,
                        func=FUNC.Identity, scale=gain, bias=shift,
                    )

        def group_h1(unit, g):
            h1_grouped[unit, g] = work.tile(
                [P, len(unit) * P, PACK], BF16, name="h1_grouped", bufs=PASSES, align_bytes=64
            )
            on_scalar = unit[-1] == TILES - 1 and g == 1
            copy = nc.scalar.copy if on_scalar else nc.vector.tensor_copy
            interleave_four(copy, h1_grouped[unit, g][:], h1[unit, g][:])

        def pack_h1(unit, g):
            width = len(unit) * P
            h1_codes[unit, g] = work.tile([P, width], U32, name="h1_codes", bufs=3, align_bytes=64)
            h1_scales[unit, g] = work.tile([P, width], U8, name="h1_scales", bufs=3, align_bytes=64)
            nc.vector.quantize_mx(
                out=h1_codes[unit, g][:].bitcast(FP8X4),
                scales=h1_scales[unit, g][:],
                in_=h1_grouped[unit, g][:].rearrange("p c t -> p (c t)"),
            )

        def second_layer(unit):
            head[unit] = psum.tile([P, len(unit), OUT], F32, name="head", bufs=1)
            for j in range(len(unit)):
                rows = slice(j * P, (j + 1) * P)
                for g in range(PASSES):
                    nc.tensor.matmul_mx(
                        out=head[unit][:, j, :],
                        lhsT=h1_codes[unit, g][:, rows].bitcast(FP8X4),
                        lhsT_scale=h1_scales[unit, g][:, rows],
                        rhs=w2_codes[:, g, :].bitcast(FP8X4),
                        rhs_scale=w2_scales[:, g, :],
                        start=(g == 0),
                        stop=(g == PASSES - 1),
                    )

        def load_base(unit):
            tiles = slice(unit[0], unit[-1] + 1)
            for name, rows in (("z", z_rows), ("k1", k1_rows)):
                state[name, unit] = work.tile([P, len(unit), OUT], BF16, name="state_" + name, bufs=2)
                nc.sync.dma_start(out=state[name, unit][:], in_=rows[:, tiles, :])

        def add_base(unit):
            width = len(unit) * OUT
            bank = psum.tile([P, len(unit), OUT], F32, name="head", bufs=1)
            flat = bank[:].rearrange("p j c -> p (j c)")
            nc.tensor.matmul(
                out=flat, lhsT=ident_bf16[:], rhs=state["z", unit][:].rearrange("p j c -> p (j c)"),
                start=True, stop=False,
            )
            nc.tensor.matmul(
                out=flat, lhsT=quarter[:], rhs=state["k1", unit][:].rearrange("p j c -> p (j c)"),
                start=False, stop=False,
            )
            nc.tensor.matmul(
                out=flat, lhsT=quarter_ones[:], rhs=b2_rows[:, 0:width], start=False, stop=True
            )
            base_bank[unit] = bank

        def copy_base(unit):
            base[unit] = work.tile([P, len(unit), OUT], F32, name="base", bufs=3)
            nc.scalar.copy(out=base[unit][:], in_=base_bank[unit][:])

        def corrector(unit):
            result = work.tile([P, len(unit), OUT], F32, name="result", bufs=2)
            nc.vector.scalar_tensor_tensor(
                out=result[:], in0=head[unit][:], scalar=STEP, in1=base[unit][:],
                op0=ALU.mult, op1=ALU.add,
            )
            nc.sync.dma_start(out=out_rows[:, unit[0] : unit[-1] + 1, :], in_=result[:])

        w1_codes, w1_scales = {}, {}
        w2_codes = keep.tile([P, PASSES, OUT], U32, name="w2_codes", align_bytes=64)
        w2_scales = keep.tile([P, PASSES, OUT], U8, name="w2_scales", align_bytes=64)
        b1_all = keep.tile([P, HID], F32, name="b1_all")
        gains = keep.tile([P, 2 * U_TILES], F32, name="gains")
        quarter = keep.tile([P, P], BF16, name="quarter")
        quarter_ones = keep.tile([P, P], BF16, name="quarter_ones")
        b2_rows = keep.tile([P, QUAD * OUT], BF16, name="b2_rows")

        with tc.tile_pool(name="prep", bufs=1) as prep:
            w1_raw = {}

            def load_w1(h):
                cols = slice(h * BANK, (h + 1) * BANK)
                for g in range(PASSES):
                    w1_raw[g, h] = prep.tile([P, PACK, BANK], BF16, name="w1_raw", bufs=PASSES * HALVES)
                    nc.sync.dma_start(
                        out=w1_raw[g, h][:],
                        in_=W1[g * K_PASS : (g + 1) * K_PASS, cols].rearrange("(p t) c -> p t c", t=PACK),
                    )

            load_h0(0, LOAD)
            load_w1(0)
            nc.sync.dma_start(out=bias_row[0:1, 0:HID], in_=b1.unsqueeze(0))
            nc.sync.dma_start(out=bias_row[0:1, HID : HID + OUT], in_=b2.unsqueeze(0))
            load_w1(1)
            w2_raw = keep.tile([P, PASSES, PACK, OUT], BF16, name="w2_raw")
            nc.scalar.dma_start(
                out=w2_raw[:], in_=W2.rearrange("(g p t) c -> p g t c", p=P, t=PACK)
            )
            for first in range(LOAD, LOADS * LOAD, LOAD):
                load_h0(first, LOAD)

            def spread_b1(h):
                cols = slice(h * BANK, (h + 1) * BANK)
                spread = psum.tile([P, BANK], F32, name="acc", bufs=ACC)
                nc.tensor.matmul(out=spread[:], lhsT=ones[:], rhs=bias_row[:, cols], start=True, stop=True)
                nc.scalar.copy(
                    out=b1_all[:, cols].rearrange("p (t m) -> p t m", t=PACK),
                    in_=spread[:].rearrange("p (m t) -> p t m", t=PACK),
                )

            w1_grouped = {}

            def regroup_w1(g, h, copy, m0=0, m1=P):
                if (g, h) not in w1_grouped:
                    w1_grouped[g, h] = prep.tile(
                        [P, BANK, PACK], BF16, name="w1_grouped", bufs=PASSES * HALVES, align_bytes=64
                    )
                copy(
                    out=w1_grouped[g, h][:].rearrange("p (t m) j -> p t m j", t=PACK)[:, :, m0:m1, :],
                    in_=w1_raw[g, h][:].rearrange("p j (m t) -> p t m j", t=PACK)[:, :, m0:m1, :],
                )

            def pack_w1(g, h):
                w1_codes[g, h] = keep.tile([P, BANK], U32, name="w1_codes", bufs=4, align_bytes=64)
                w1_scales[g, h] = keep.tile([P, BANK], U8, name="w1_scales", bufs=4, align_bytes=64)
                nc.vector.quantize_mx(
                    out=w1_codes[g, h][:].bitcast(FP8X4), scales=w1_scales[g, h][:],
                    in_=w1_grouped[g, h][:].rearrange("p c t -> p (c t)"),
                )

            turn_h0(0)
            group_h0(0, nc.vector.tensor_copy)
            turn_h0(1)
            group_h0(1, nc.scalar.copy)
            pack_h0(0)
            regroup_w1(1, 0, nc.scalar.copy, 0, 64)
            regroup_w1(0, 0, nc.vector.tensor_copy)
            pack_h0(1)
            pack_w1(0, 0)
            regroup_w1(1, 0, nc.vector.tensor_copy, 64, P)
            pack_w1(1, 0)
            spread_b1(0)
            spread_b1(1)
            first_layer(0, [0])
            first_layer(1, [0])
            regroup_w1(1, 1, nc.scalar.copy, 0, 96)
            regroup_w1(0, 1, nc.vector.tensor_copy)
            pack_w1(0, 1)
            add_bias(0, [0])
            regroup_w1(1, 1, nc.vector.tensor_copy, 96, P)
            add_bias(1, [0])
            pack_w1(1, 1)
            turn_h0(2)
            group_h0(2, nc.scalar.copy)
            turn_h0(3)
            group_h0(3, nc.scalar.copy)
        def prepare_w2():
            w2_grouped = work.tile([P, PASSES, OUT, PACK], BF16, name="w2_grouped", align_bytes=64)
            for g in range(PASSES):
                interleave_four(nc.vector.tensor_copy, w2_grouped[:, g, :, :], w2_raw[:, g, :, :])
            nc.vector.quantize_mx(
                out=w2_codes[:].rearrange("p g c -> p (g c)").bitcast(FP8X4),
                scales=w2_scales[:].rearrange("p g c -> p (g c)"),
                in_=w2_grouped[:].rearrange("p g c t -> p (g c t)"),
            )
            nc.vector.tensor_scalar_mul(quarter[:], ident_bf16[:], STEP)
            nc.vector.memset(quarter_ones[:], STEP)
            for j in range(QUAD):
                nc.vector.tensor_copy(
                    out=b2_rows[:, j * OUT : (j + 1) * OUT], in_=bias_row[:, HID : HID + OUT]
                )
            for v, rows in enumerate((gain_rows, shift_rows)):
                nc.vector.tensor_copy(
                    out=gains[:, v * U_TILES : (v + 1) * U_TILES],
                    in_=rows[:].rearrange("p g t -> p (g t)"),
                )
        work = ctx.enter_context(tc.tile_pool(name="work", bufs=1))

        def live(n):
            return 0 <= n < TILES

        def turn(n):
            if live(n):
                turn_h0(n)

        def group(n, copy):
            if live(n):
                group_h0(n, copy)


        def live(n):
            return 0 <= n < TILES

        def turn(n):
            if live(n):
                turn_h0(n)

        def group(n, copy):
            if live(n):
                group_h0(n, copy)

        def pack(n):
            if live(n):
                pack_h0(n)

        def multiply(n):
            if live(n):
                first_layer(n)

        first_group = [8, 8, 8, 8][0]
        exponential_half(0, 0)
        exponential_half(1, 0)
        for n in range(4, 6):
            turn_h0(n)
            group_h0(n, nc.scalar.copy)
        for n in range(2):
            first_layer(n, [1])
        for n in range(6, 8):
            turn_h0(n)
            group_h0(n, nc.scalar.copy)
        pack_h0(2)
        add_bias(0, [1])
        exponential_half(0, 1)
        pack_h0(3)
        first_layer(2)
        add_bias(1, [1])
        exponential_half(1, 1)
        for n in range(2, first_group):
            if n + 2 < 8:
                pack_h0(n + 2)
            if n + 1 < 8:
                first_layer(n + 1)
            add_bias(n)
            exponential(n)
        for n in range(first_group):
            softplus(n)
        prepare_w2()
        added = first_group + LEAD
        for n in range(4, added):
            if n + 4 >= 8:
                turn(n + 4)
            if n + 3 >= 8:
                group(n + 3, nc.vector.tensor_copy)
            if n + 1 >= min(first_group + 1, 8):
                multiply(n + 1)
            if n >= first_group:
                add_bias(n)
            if n + 2 >= min(first_group + 2, 8):
                pack(n + 2)

        groups = [8, 8, 8, 8]
        per_step = [[] for n in range(TILES)]
        first = 0
        for g, size in enumerate(groups):
            acts = []
            follow = groups[g + 1] if g + 1 < len(groups) else 0
            x = [(tanh, first + j) for j in range(size)]
            y = [(exponential, first + size + j) for j in range(follow)]
            for j in range(max(size, follow)):
                acts += x[j : j + 1] + y[j : j + 1]
            acts += [(softplus, first + size + j) for j in range(follow)]
            if g == len(groups) - 2:
                acts.append((tanh, first + size))
            if g == len(groups) - 1:
                acts = acts[1:]
                for j in range(size - 1):
                    per_step[first + j] = acts[j : j + 1]
                continue
            for j in range(size):
                per_step[first + j] = acts[j * len(acts) // size : (j + 1) * len(acts) // size]
            first += size

        units = [range(n, n + QUAD) for n in range(0, TILES - QUAD, QUAD)]
        units += [range(TILES - QUAD, TILES - 2), range(TILES - 2, TILES)]
        starts = [unit[-1] + 4 for unit in units[:-2]]
        starts += [starts[-1] + QUAD, starts[-1] + QUAD + 2]

        def banks_of(i):
            return [
                (unit, 2 * (i - start) + b)
                for unit, start in zip(units, starts)
                for b in range(2)
                if 0 <= i - start < len(unit)
            ]

        def vector_takes(i, k):
            if live(i + added):
                return k == 1 and i % 2 == 0
            if live(i + groups[-1]):
                return k == 1 and (i % 2 == 1 or i == 22)
            return k == 1 and i % 2 == 1 and i < 32

        def work_on_head(i, lag, stage):
            for unit, start in zip(units, starts):
                if i == start + lag(len(unit)):
                    stage(unit)

        for i in range(starts[-1] + len(units[-1]) + 3):
            a = i + added
            early = live(a)
            now = per_step[i] if live(i) else []
            banks = banks_of(i)
            vector_banks = [k for k in range(len(banks)) if vector_takes(i, k)]
            work_on_head(i, lambda w: -2, load_base)
            for k in range(max(len(now), len(banks))):
                if k < len(now):
                    stage, n = now[k]
                    stage(n)
                if k == min(1, len(now)) and live(i - 1) and squares_on_scalar(i - 1):
                    sum_squares(i - 1)
                if k < len(banks) and k not in vector_banks:
                    scale_act(*banks[k], False)
            work_on_head(i, lambda w: 1, copy_base)
            def early_step():
                if live(i - 3):
                    offset(i - 3)
                    normalise_on_gpsimd(i - 3)
                mish(i)
                if live(i - 1):
                    partial_statistics(i - 1)
                for unit, bank in banks_of(i + 1):
                    turn_act(unit, bank)
                work_on_head(i, lambda w: 0, add_base)
                add_bias(a, [0])
                if live(i - 1):
                    aggregate(i - 1)
                add_bias(a, [1])
                if live(i - 1):
                    shift(i - 1)
                    if (i - 1) % PAIR == PAIR - 1:
                        root_pair((i - 1) // PAIR)
                for k in vector_banks:
                    scale_act(*banks[k], True)
                multiply(a + 1)
                group(a + 3, nc.vector.tensor_copy)
                work_on_head(i, lambda w: w + 2, corrector)
                turn(a + 4)
                pack(a + 2)
                head_work()
                mish_rest(i)

            def head_work():
                work_on_head(i, lambda w: w // 2 + 1, lambda u: pack_h1(u, 0))
                work_on_head(i, lambda w: w + 1, lambda u: pack_h1(u, 1))
                work_on_head(i, lambda w: w + 1, second_layer)
                work_on_head(i, lambda w: w // 2, lambda u: group_h1(u, 0))
                work_on_head(i, lambda w: w, lambda u: group_h1(u, 1))

            def late_step():
                n = i - 3
                on_g = live(n) and gpsimd_normalises(n)
                counted = live(i - 1) and not squares_on_scalar(i - 1)
                root_now = n % PAIR == 0 and n >= TILES - added - PAIR and live(n)
                if root_now:
                    root_pair(n // PAIR)
                elif on_g:
                    offset(n)
                    normalise_on_gpsimd(n)
                if live(i):
                    mish(i)
                if counted:
                    partial_statistics(i - 1)
                if counted and not root_now:
                    aggregate(i - 1)
                for k in vector_banks:
                    scale_act(*banks[k], True)
                if counted and root_now:
                    aggregate(i - 1)
                if root_now and on_g:
                    offset(n)
                    normalise_on_gpsimd(n)
                if live(i):
                    mish_rest(i)
                if counted:
                    shift(i - 1)
                if live(n) and not on_g:
                    normalise_on_vector(n)
                if live(i) and squares_on_scalar(i):
                    find_mean(i)
                for unit, bank in banks_of(i + 1):
                    turn_act(unit, bank)
                work_on_head(i, lambda w: 0, add_base)
                work_on_head(i, lambda w: w + 2, corrector)
                head_work()
                if live(i - 1) and squares_on_scalar(i - 1):
                    shift(i - 1)

            if early:
                early_step()
            else:
                late_step()
